import numpy as np
import ml_dtypes


def mxq(x, axis, fmt="e4m3"):
    dtype, down = {"e4m3": (ml_dtypes.float8_e4m3fn, 7), "e5m2": (ml_dtypes.float8_e5m2, 14)}[fmt]
    v = np.moveaxis(np.asarray(x, np.float32).astype(ml_dtypes.bfloat16).astype(np.float64), axis, -1)
    blocks = v.reshape(v.shape[:-1] + (-1, 32))
    amax = np.abs(blocks).max(-1, keepdims=True)
    byte = np.maximum(np.where(amax > 0, np.frexp(amax)[1] - 1 + 127, 0) - down, 1)
    scale = np.exp2(byte - 127.0)
    codes = (blocks / scale).astype(np.float32).astype(dtype).astype(np.float64)
    return np.moveaxis((codes * scale).reshape(v.shape), -1, axis)


WIDE = False


def mx_kscale(k):
    if not WIDE:
        return np.ones(k)
    levels = np.array([10, -10, 5, -5, 0])
    a = np.random.permutation(np.resize(levels, k // 512 * 4)).reshape(k // 512, 4)
    idx = np.arange(k)
    return np.exp2(a[idx // 512, idx % 128 // 32])


BF16 = ml_dtypes.bfloat16


def bf(x):
    return np.asarray(x, np.float32).astype(BF16)


def f64(x):
    return np.asarray(x).astype(np.float64)


E2M1 = np.array([0.0, 0.5, 1.0, 1.5, 2.0, 3.0, 4.0, 6.0, -0.0, -0.5, -1.0, -1.5, -2.0, -3.0, -4.0, -6.0])


def pack_weight(w, fmt):
    k, n = w.shape
    w = f64(bf(w)).reshape(k // 32, 32, n)
    amax = np.abs(w).max(1)
    if fmt == "e4m3":
        byte = np.frexp(amax)[1] - 1 + 127 - 7
    else:
        mant, ex = np.frexp(amax / 6.0)
        byte = np.where(mant > 0.5, ex, ex - 1) + 127
    byte = np.clip(np.where(amax > 0, byte, 1), 1, 254)
    scaled = (w * np.exp2(127.0 - byte)[:, None, :]).reshape(k, n).astype(np.float32)
    by_word = np.ascontiguousarray(scaled.reshape(k // 512, 128, 4, n).transpose(0, 1, 3, 2))
    if fmt == "e4m3":
        words = by_word.astype(ml_dtypes.float8_e4m3fn).view(np.uint8)
    else:
        c = by_word.astype(ml_dtypes.float4_e2m1fn).view(np.uint8) & 0xF
        words = c[..., 0::2] | (c[..., 1::2] << 4)
    return np.ascontiguousarray(words), np.ascontiguousarray(byte.astype(np.uint8).reshape(k // 512, 16, n))


def unpack_weight(words, scales, fmt):
    g, p, n, _ = words.shape
    if fmt == "e4m3":
        vals = np.ascontiguousarray(words).view(ml_dtypes.float8_e4m3fn).astype(np.float64)
    else:
        nib = np.empty((g, p, n, 4), np.uint8)
        nib[..., 0::2] = words & 0xF
        nib[..., 1::2] = words >> 4
        vals = E2M1[nib]
    vals = vals * np.repeat(np.exp2(scales.astype(np.float64) - 127.0), 8, axis=1)[..., None]
    return vals.transpose(0, 1, 3, 2).reshape(g * 512, n)


B, F, Hg, Wg, D, NH, HD = 1, 8, 32, 32, 512, 1, 128
N = F * Hg * Wg
E = NH * HD
DIM_BASE = HD // 6
DIM_H = 2 * DIM_BASE
DIM_W = 2 * DIM_BASE
DIM_T = HD - DIM_H - DIM_W
EPS = 1e-6
THETA = 10000.0
FMT = "e4m3"


def make_freqs(n_pos, dim):
    half = dim // 2
    inv = 1.0 / THETA ** (np.arange(half) / half)
    ang = np.arange(n_pos)[:, None] * inv[None, :]
    return np.stack([np.cos(ang), np.sin(ang)], axis=-1)


def rms_norm(v, gain):
    var = np.mean(np.square(v), axis=-1, keepdims=True)
    return v * (1.0 / np.sqrt(var + EPS)) * gain


def rope_apply(v, freqs_t, freqs_h, freqs_w):
    fg = np.concatenate([
        np.broadcast_to(freqs_t[:, None, None, :, :], (F, Hg, Wg, DIM_T // 2, 2)),
        np.broadcast_to(freqs_h[None, :, None, :, :], (F, Hg, Wg, DIM_H // 2, 2)),
        np.broadcast_to(freqs_w[None, None, :, :, :], (F, Hg, Wg, DIM_W // 2, 2)),
    ], axis=3).reshape(N, HD // 2, 2)[None, :, None, :, :]
    vc = v.reshape(B, N, NH, HD // 2, 2)
    out = np.stack([
        vc[..., 0] * fg[..., 0] - vc[..., 1] * fg[..., 1],
        vc[..., 0] * fg[..., 1] + vc[..., 1] * fg[..., 0],
    ], axis=-1)
    return out.reshape(B, N, NH, HD)


def setup_inputs():
    s = mx_kscale(D)
    x = bf(np.random.standard_normal((B, N, D)) * s)
    Wq_words, Wq_scales = pack_weight(np.random.standard_normal((D, E)) / np.sqrt(D) / s[:, None], FMT)
    bq = bf(np.random.standard_normal(E) * 0.1)
    Wk_words, Wk_scales = pack_weight(np.random.standard_normal((D, E)) / np.sqrt(D) / s[:, None], FMT)
    bk = bf(np.random.standard_normal(E) * 0.1)
    return {
        "x": x,
        "Wq_words": Wq_words,
        "Wq_scales": Wq_scales,
        "bq": bq,
        "Wk_words": Wk_words,
        "Wk_scales": Wk_scales,
        "bk": bk,
        "q_scale": bf(1.0 + 0.1 * np.random.standard_normal(HD)),
        "k_scale": bf(1.0 + 0.1 * np.random.standard_normal(HD)),
        "freqs_t": bf(make_freqs(F, DIM_T)),
        "freqs_h": bf(make_freqs(Hg, DIM_H)),
        "freqs_w": bf(make_freqs(Wg, DIM_W)),
    }


def reference(x, Wq_words, Wq_scales, bq, Wk_words, Wk_scales, bk, q_scale, k_scale, freqs_t, freqs_h, freqs_w):
    xq = mxq(f64(x), 2, "e4m3")
    q = ((xq @ unpack_weight(Wq_words, Wq_scales, FMT)) + f64(bq)).reshape(B, N, NH, HD)
    k = ((xq @ unpack_weight(Wk_words, Wk_scales, FMT)) + f64(bk)).reshape(B, N, NH, HD)
    q = rms_norm(q, f64(q_scale))
    k = rms_norm(k, f64(k_scale))
    q_rot = rope_apply(q, f64(freqs_t), f64(freqs_h), f64(freqs_w))
    k_rot = rope_apply(k, f64(freqs_t), f64(freqs_h), f64(freqs_w))
    return q_rot, k_rot

@@ -1,0 +1,242 @@
+from contextlib import ExitStack
+
+import concourse.mybir as mybir
+from concourse.masks import make_identity
+
+F32 = mybir.dt.float32
+BF16 = mybir.dt.bfloat16
+I32 = mybir.dt.int32
+U32 = mybir.dt.uint32
+U8 = mybir.dt.uint8
+FP8X4 = mybir.dt.float8_e4m3fn_x4
+ACT = mybir.ActivationFunctionType
+ALU = mybir.AluOpType
+
+P = 128
+D = 512
+HD = 128
+PAIRS = HD // 2
+FRAMES = 8
+SLOTS = 8
+GROUP = 4
+HALF = 2
+PAIRS_T = 22
+PAIRS_H = 21
+PAIRS_W = 21
+PAIRS_HW = PAIRS_H + PAIRS_W
+EPS = 1e-6
+
+FLOPS = 2 * 8192 * D * 2 * HD
+
+
+def tile_multiheadattention_pa_t_kernel(
+    tc, x, Wq_words, Wq_scales, bq, Wk_words, Wk_scales, bk, q_scale, k_scale,
+    freqs_t, freqs_h, freqs_w, out_0, out_1,
+):
+    nc = tc.nc
+    x_frames = x.rearrange("b (t p j) d -> (b t) p j d", p=P, j=SLOTS)
+    out_frames = [
+        o.rearrange("b (t p j) h f -> (b t) p j (h f)", p=P, j=SLOTS) for o in (out_0, out_1)
+    ]
+
+    with ExitStack() as ctx:
+        consts = ctx.enter_context(tc.tile_pool(name="consts", bufs=1))
+        stream = ctx.enter_context(tc.tile_pool(name="stream", bufs=3))
+        psum = ctx.enter_context(tc.psum_pool(name="psum", bufs=2))
+
+        w_codes = consts.tile([P, 2, HD], U32, align_bytes=64)
+        w_planes = consts.tile([P, 2, HD], U8, align_bytes=64)
+        nc.vector.memset(w_planes[:].rearrange("p a n -> p (a n)").bitcast(I32), 0)
+        for qk, (words, scales) in enumerate(((Wq_words, Wq_scales), (Wk_words, Wk_scales))):
+            nc.sync.dma_start(
+                out=w_codes[:, qk, :].bitcast(I32),
+                in_=words.rearrange("g p n t -> (g p) (n t)").bitcast(I32),
+            )
+            for quad in range(4):
+                nc.sync.dma_start(
+                    out=w_planes[32 * quad : 32 * quad + 4, qk, :].bitcast(I32),
+                    in_=scales[0, 4 * quad : 4 * quad + 4, :].bitcast(I32),
+                )
+
+        ident = consts.tile([P, P], F32)
+        make_identity(nc, ident[:])
+
+        bias_rows = consts.tile([P, HD], BF16)
+        nc.vector.memset(bias_rows[:], 0.0)
+        nc.scalar.dma_start(out=bias_rows[0:1, :], in_=bq.unsqueeze(0))
+        nc.scalar.dma_start(out=bias_rows[1:2, :], in_=bk.unsqueeze(0))
+        bias_rows_f32 = consts.tile([P, HD], F32)
+        nc.vector.tensor_copy(out=bias_rows_f32[:], in_=bias_rows[:])
+        bias_ps = psum.tile([P, HALF, 2, HD], F32, tag="v", bufs=4)
+        nc.tensor.transpose(bias_ps[:, 0, 0, :], bias_rows_f32[:], ident[:])
+        bias_col = consts.tile([P, 2], F32)
+        nc.vector.tensor_copy(out=bias_col[:], in_=bias_ps[:, 0, 0, 0:2])
+
+        eps_col = consts.tile([P, 1], F32)
+        nc.vector.memset(eps_col[:], EPS)
+
+        gains = consts.tile([P, 2, HD], BF16)
+        nc.scalar.dma_start(out=gains[:, 0, :], in_=q_scale.partition_broadcast(P))
+        nc.scalar.dma_start(out=gains[:, 1, :], in_=k_scale.partition_broadcast(P))
+        cs_t = consts.tile([P, FRAMES, PAIRS_T, 2], BF16)
+        nc.scalar.dma_start(
+            out=cs_t[:].rearrange("p t a b -> p (t a b)"),
+            in_=freqs_t.rearrange("t a b -> (t a b)").partition_broadcast(P),
+        )
+        cs_h = consts.tile([P, PAIRS_H, 2], BF16)
+        nc.scalar.dma_start(
+            out=cs_h[:].rearrange("p a b -> p (a b)"),
+            in_=freqs_h.rearrange("h a b -> h (a b)").unsqueeze(1).to_broadcast([32, 4, 2 * PAIRS_H]),
+        )
+        cs_w = consts.tile([P, SLOTS, PAIRS_W, 2], BF16)
+        nc.scalar.dma_start(
+            out=cs_w[:].rearrange("p j a b -> p (j a b)"),
+            in_=freqs_w.rearrange("(wh j) a b -> wh (j a b)", j=SLOTS)
+            .unsqueeze(0)
+            .to_broadcast([32, 4, SLOTS * 2 * PAIRS_W]),
+        )
+
+        table_t = consts.tile([P, FRAMES, 2, 2, 2, PAIRS_T], F32)
+        table_hw = consts.tile([P, SLOTS, 2, 2, 2, PAIRS_HW], F32)
+        for qk in range(2):
+            gain_pairs = gains[:, qk, :].rearrange("p (pr two) -> p pr two", two=2)
+            for src in range(2):
+                for e in range(2):
+                    pick = e ^ src
+                    sign = -1.0 if (src == 1 and e == 0) else 1.0
+                    nc.vector.scalar_tensor_tensor(
+                        out=table_t[:, :, qk, src, e, :],
+                        in0=cs_t[:, :, :, pick],
+                        scalar=sign,
+                        in1=gain_pairs[:, 0:PAIRS_T, src].unsqueeze(1).to_broadcast([P, FRAMES, PAIRS_T]),
+                        op0=ALU.mult,
+                        op1=ALU.mult,
+                    )
+                    nc.vector.scalar_tensor_tensor(
+                        out=table_hw[:, :, qk, src, e, 0:PAIRS_H],
+                        in0=cs_h[:, :, pick].unsqueeze(1).to_broadcast([P, SLOTS, PAIRS_H]),
+                        scalar=sign,
+                        in1=gain_pairs[:, PAIRS_T : PAIRS_T + PAIRS_H, src]
+                        .unsqueeze(1)
+                        .to_broadcast([P, SLOTS, PAIRS_H]),
+                        op0=ALU.mult,
+                        op1=ALU.mult,
+                    )
+                    nc.vector.scalar_tensor_tensor(
+                        out=table_hw[:, :, qk, src, e, PAIRS_H:PAIRS_HW],
+                        in0=cs_w[:, :, :, pick],
+                        scalar=sign,
+                        in1=gain_pairs[:, PAIRS_T + PAIRS_H : PAIRS, src]
+                        .unsqueeze(1)
+                        .to_broadcast([P, SLOTS, PAIRS_W]),
+                        op0=ALU.mult,
+                        op1=ALU.mult,
+                    )
+
+        for t in range(FRAMES):
+            for j0 in range(0, SLOTS, GROUP):
+                x_sb = stream.tile([P, GROUP, D], BF16, bufs=4)
+                nc.sync.dma_start(out=x_sb[:], in_=x_frames[t, :, j0 : j0 + GROUP, :])
+
+                grouped = stream.tile([P, GROUP * P, 2, 2], BF16, align_bytes=64)
+                grouped_words = grouped[:].rearrange("p n u e -> p (n u e)").bitcast(F32)
+                for half in range(GROUP // HALF):
+                    x_t = psum.tile([P, 2, HALF * P], F32, tag="x_t", bufs=2)
+                    for s in range(HALF):
+                        words = x_sb[:, half * HALF + s, :].bitcast(F32)
+                        for u in range(2):
+                            nc.tensor.transpose(
+                                x_t[:, u, s * P : (s + 1) * P], words[:, u : D // 2 : 2], ident[:]
+                            )
+                    nc.scalar.copy(
+                        out=grouped_words[:, half * HALF * P * 2 : (half + 1) * HALF * P * 2].rearrange(
+                            "p (n u) -> p n u", u=2
+                        ),
+                        in_=x_t[:].rearrange("p u n -> p n u"),
+                    )
+
+                x_codes = stream.tile([P, GROUP * P], U32, align_bytes=64)
+                x_planes = stream.tile([P, GROUP * P], U8, align_bytes=64)
+                nc.vector.quantize_mx(
+                    out=x_codes[:].bitcast(FP8X4),
+                    scales=x_planes[:],
+                    in_=grouped[:].rearrange("p n u e -> p (n u e)"),
+                )
+
+                v_t = stream.tile([P, 2, GROUP * P], F32)
+                for qk in range(2):
+                    acc = psum.tile([P, GROUP * P], F32, tag="acc", bufs=2)
+                    nc.tensor.matmul_mx(
+                        out=acc[:],
+                        lhsT=w_codes[:, qk, :].bitcast(FP8X4),
+                        lhsT_scale=w_planes[:, qk, :],
+                        rhs=x_codes[:].bitcast(FP8X4),
+                        rhs_scale=x_planes[:],
+                        start=True,
+                        stop=True,
+                    )
+                    nc.scalar.activation(
+                        out=v_t[:, qk, :], in_=acc[:], func=ACT.Identity, bias=bias_col[:, qk : qk + 1]
+                    )
+
+                v_banks = []
+                for half in range(GROUP // HALF):
+                    v = psum.tile([P, HALF, 2, HD], F32, tag="v", bufs=4)
+                    v_banks.append(v)
+                    for s in range(HALF):
+                        for qk in range(2):
+                            col = (half * HALF + s) * P
+                            nc.tensor.transpose(v[:, s, qk, :], v_t[:, qk, col : col + P], ident[:])
+
+                sumsq = stream.tile([P, GROUP, 2], F32)
+                squares = stream.tile([P, GROUP, 2, HD], BF16, bufs=2)
+                for s in range(GROUP):
+                    for qk in range(2):
+                        nc.scalar.activation(
+                            out=squares[:, s, qk, :],
+                            in_=v_banks[s // HALF][:, s % HALF, qk, :],
+                            func=ACT.Square,
+                            accum_out=sumsq[:, s, qk : qk + 1],
+                        )
+                rms = stream.tile([P, GROUP, 2], F32)
+                nc.scalar.activation(
+                    out=rms[:], in_=sumsq[:], func=ACT.Sqrt, bias=eps_col[:, 0:1], scale=1.0 / HD
+                )
+                rstd = stream.tile([P, GROUP, 2], F32)
+                nc.vector.reciprocal(out=rstd[:], in_=rms[:])
+
+                products = stream.tile([P, 2, 2, GROUP, 2, PAIRS], F32)
+                for s in range(GROUP):
+                    for qk in range(2):
+                        v_pairs = v_banks[s // HALF][:, s % HALF, qk, :].rearrange(
+                            "p (pr two) -> p two pr", two=2
+                        )
+                        for src in range(2):
+                            nc.vector.scalar_tensor_tensor(
+                                out=products[:, src, qk, s, :, 0:PAIRS_T],
+                                in0=v_pairs[:, src, 0:PAIRS_T].unsqueeze(1).to_broadcast([P, 2, PAIRS_T]),
+                                scalar=rstd[:, s, qk : qk + 1],
+                                in1=table_t[:, t, qk, src, :, :],
+                                op0=ALU.mult,
+                                op1=ALU.mult,
+                            )
+                            nc.vector.scalar_tensor_tensor(
+                                out=products[:, src, qk, s, :, PAIRS_T:PAIRS],
+                                in0=v_pairs[:, src, PAIRS_T:PAIRS].unsqueeze(1).to_broadcast([P, 2, PAIRS_HW]),
+                                scalar=rstd[:, s, qk : qk + 1],
+                                in1=table_hw[:, j0 + s, qk, src, :, :],
+                                op0=ALU.mult,
+                                op1=ALU.mult,
+                            )
+
+                rotated = stream.tile([P, 2, GROUP, HD], F32)
+                for qk in range(2):
+                    nc.gpsimd.tensor_tensor(
+                        out=rotated[:, qk, :, :].rearrange("p s (pr e) -> p s pr e", e=2),
+                        in0=products[:, 0, qk, :, :, :].rearrange("p s e pr -> p s pr e"),
+                        in1=products[:, 1, qk, :, :, :].rearrange("p s e pr -> p s pr e"),
+                        op=ALU.add,
+                    )
+                    nc.sync.dma_start(
+                        out=out_frames[qk][t, :, j0 : j0 + GROUP, :], in_=rotated[:, qk, :, :]
+                    )

@@ -20,10 +20,15 @@ FRAMES = 8
 SLOTS = 8
 GROUP = 4
 HALF = 2
+HALVES = GROUP // HALF
+LOADS_AHEAD = 3
 PAIRS_T = 22
 PAIRS_H = 21
 PAIRS_W = 21
 PAIRS_HW = PAIRS_H + PAIRS_W
+FEAT_T = 2 * PAIRS_T
+FEAT_H = 2 * PAIRS_H
+FEAT_W = 2 * PAIRS_W
 EPS = 1e-6
 
 FLOPS = 2 * 8192 * D * 2 * HD
@@ -78,9 +83,9 @@ def tile_multiheadattention_pa_t_kernel(
         gains = consts.tile([P, 2, HD], BF16)
         nc.scalar.dma_start(out=gains[:, 0, :], in_=q_scale.partition_broadcast(P))
         nc.scalar.dma_start(out=gains[:, 1, :], in_=k_scale.partition_broadcast(P))
-        cs_t = consts.tile([P, FRAMES, PAIRS_T, 2], BF16)
+        cs_t = consts.tile([P, FRAMES * PAIRS_T, 2], BF16)
         nc.scalar.dma_start(
-            out=cs_t[:].rearrange("p t a b -> p (t a b)"),
+            out=cs_t[:].rearrange("p a b -> p (a b)"),
             in_=freqs_t.rearrange("t a b -> (t a b)").partition_broadcast(P),
         )
         cs_h = consts.tile([P, PAIRS_H, 2], BF16)
@@ -88,155 +93,218 @@ def tile_multiheadattention_pa_t_kernel(
             out=cs_h[:].rearrange("p a b -> p (a b)"),
             in_=freqs_h.rearrange("h a b -> h (a b)").unsqueeze(1).to_broadcast([32, 4, 2 * PAIRS_H]),
         )
-        cs_w = consts.tile([P, SLOTS, PAIRS_W, 2], BF16)
+        cs_w = consts.tile([P, SLOTS * PAIRS_W, 2], BF16)
         nc.scalar.dma_start(
-            out=cs_w[:].rearrange("p j a b -> p (j a b)"),
+            out=cs_w[:].rearrange("p a b -> p (a b)"),
             in_=freqs_w.rearrange("(wh j) a b -> wh (j a b)", j=SLOTS)
             .unsqueeze(0)
             .to_broadcast([32, 4, SLOTS * 2 * PAIRS_W]),
         )
 
-        table_t = consts.tile([P, FRAMES, 2, 2, 2, PAIRS_T], F32)
-        table_hw = consts.tile([P, SLOTS, 2, 2, 2, PAIRS_HW], F32)
-        for qk in range(2):
-            gain_pairs = gains[:, qk, :].rearrange("p (pr two) -> p pr two", two=2)
-            for src in range(2):
-                for e in range(2):
-                    pick = e ^ src
-                    sign = -1.0 if (src == 1 and e == 0) else 1.0
-                    nc.vector.scalar_tensor_tensor(
-                        out=table_t[:, :, qk, src, e, :],
-                        in0=cs_t[:, :, :, pick],
-                        scalar=sign,
-                        in1=gain_pairs[:, 0:PAIRS_T, src].unsqueeze(1).to_broadcast([P, FRAMES, PAIRS_T]),
-                        op0=ALU.mult,
-                        op1=ALU.mult,
-                    )
-                    nc.vector.scalar_tensor_tensor(
-                        out=table_hw[:, :, qk, src, e, 0:PAIRS_H],
-                        in0=cs_h[:, :, pick].unsqueeze(1).to_broadcast([P, SLOTS, PAIRS_H]),
-                        scalar=sign,
-                        in1=gain_pairs[:, PAIRS_T : PAIRS_T + PAIRS_H, src]
-                        .unsqueeze(1)
-                        .to_broadcast([P, SLOTS, PAIRS_H]),
-                        op0=ALU.mult,
-                        op1=ALU.mult,
-                    )
-                    nc.vector.scalar_tensor_tensor(
-                        out=table_hw[:, :, qk, src, e, PAIRS_H:PAIRS_HW],
-                        in0=cs_w[:, :, :, pick],
-                        scalar=sign,
-                        in1=gain_pairs[:, PAIRS_T + PAIRS_H : PAIRS, src]
-                        .unsqueeze(1)
-                        .to_broadcast([P, SLOTS, PAIRS_W]),
-                        op0=ALU.mult,
-                        op1=ALU.mult,
-                    )
+        sc_t = consts.tile([P, FRAMES * PAIRS_T, 2], BF16)
+        sc_h = consts.tile([P, PAIRS_H, 2], BF16)
+        sc_w = consts.tile([P, SLOTS * PAIRS_W, 2], BF16)
+        for swapped, given in ((sc_t, cs_t), (sc_h, cs_h), (sc_w, cs_w)):
+            for i in range(2):
+                nc.vector.tensor_copy(out=swapped[:, :, i], in_=given[:, :, 1 - i])
+        signed_gains = consts.tile([P, 2, 2, PAIRS, 2], F32)
+        gain_pairs = gains[:].rearrange("p q (pr two) -> p q pr two", two=2)
+        nc.vector.tensor_copy(out=signed_gains[:, 0, :, :, 0], in_=gain_pairs[:, :, :, 0])
+        nc.vector.tensor_scalar_mul(out=signed_gains[:, 0, :, :, 1], in0=gain_pairs[:, :, :, 1], scalar1=-1.0)
+        nc.vector.tensor_copy(out=signed_gains[:, 1, :, :, :], in_=gain_pairs)
 
-        for t in range(FRAMES):
-            for j0 in range(0, SLOTS, GROUP):
-                x_sb = stream.tile([P, GROUP, D], BF16, bufs=4)
-                nc.sync.dma_start(out=x_sb[:], in_=x_frames[t, :, j0 : j0 + GROUP, :])
+        table_t = consts.tile([P, FRAMES, 2, 2, 2 * PAIRS_T], F32)
+        table_hw = consts.tile([P, SLOTS, 2, 2, 2 * PAIRS_HW], F32)
 
-                grouped = stream.tile([P, GROUP * P, 2, 2], BF16, align_bytes=64)
-                grouped_words = grouped[:].rearrange("p n u e -> p (n u e)").bitcast(F32)
-                for half in range(GROUP // HALF):
-                    x_t = psum.tile([P, 2, HALF * P], F32, tag="x_t", bufs=2)
-                    for s in range(HALF):
-                        words = x_sb[:, half * HALF + s, :].bitcast(F32)
-                        for u in range(2):
-                            nc.tensor.transpose(
-                                x_t[:, u, s * P : (s + 1) * P], words[:, u : D // 2 : 2], ident[:]
-                            )
-                    nc.scalar.copy(
-                        out=grouped_words[:, half * HALF * P * 2 : (half + 1) * HALF * P * 2].rearrange(
-                            "p (n u) -> p n u", u=2
-                        ),
-                        in_=x_t[:].rearrange("p u n -> p n u"),
-                    )
-
-                x_codes = stream.tile([P, GROUP * P], U32, align_bytes=64)
-                x_planes = stream.tile([P, GROUP * P], U8, align_bytes=64)
-                nc.vector.quantize_mx(
-                    out=x_codes[:].bitcast(FP8X4),
-                    scales=x_planes[:],
-                    in_=grouped[:].rearrange("p n u e -> p (n u e)"),
+        def build_tables(qk):
+            for e, (turn_t, turn_h, turn_w) in enumerate(((cs_t, cs_h, cs_w), (sc_t, sc_h, sc_w))):
+                gain = signed_gains[:, e, qk, :, :].rearrange("p pr two -> p (pr two)")
+                nc.vector.tensor_tensor(
+                    out=table_t[:, :, qk, e, :],
+                    in0=turn_t[:].rearrange("p (t a) b -> p t (a b)", t=FRAMES),
+                    in1=gain[:, 0:FEAT_T].unsqueeze(1).to_broadcast([P, FRAMES, FEAT_T]),
+                    op=ALU.mult,
+                )
+                nc.vector.tensor_tensor(
+                    out=table_hw[:, :, qk, e, 0:FEAT_H],
+                    in0=turn_h[:].rearrange("p a b -> p (a b)").unsqueeze(1).to_broadcast([P, SLOTS, FEAT_H]),
+                    in1=gain[:, FEAT_T : FEAT_T + FEAT_H].unsqueeze(1).to_broadcast([P, SLOTS, FEAT_H]),
+                    op=ALU.mult,
+                )
+                nc.vector.tensor_tensor(
+                    out=table_hw[:, :, qk, e, FEAT_H : FEAT_H + FEAT_W],
+                    in0=turn_w[:].rearrange("p (j a) b -> p j (a b)", j=SLOTS),
+                    in1=gain[:, FEAT_T + FEAT_H : HD].unsqueeze(1).to_broadcast([P, SLOTS, FEAT_W]),
+                    op=ALU.mult,
                 )
 
-                v_t = stream.tile([P, 2, GROUP * P], F32)
-                for qk in range(2):
-                    acc = psum.tile([P, GROUP * P], F32, tag="acc", bufs=2)
-                    nc.tensor.matmul_mx(
-                        out=acc[:],
-                        lhsT=w_codes[:, qk, :].bitcast(FP8X4),
-                        lhsT_scale=w_planes[:, qk, :],
-                        rhs=x_codes[:].bitcast(FP8X4),
-                        rhs_scale=x_planes[:],
-                        start=True,
-                        stop=True,
-                    )
-                    nc.scalar.activation(
-                        out=v_t[:, qk, :], in_=acc[:], func=ACT.Identity, bias=bias_col[:, qk : qk + 1]
-                    )
+        groups = [(t, j0) for t in range(FRAMES) for j0 in range(0, SLOTS, GROUP)]
+        n_groups = len(groups)
+        x_tiles, x_t_banks, grouped_tiles, x_mx, acc_banks, v_t_tiles = {}, {}, {}, {}, {}, {}
+        v_banks, rms_tiles, rstd_tiles, product_tiles, rotated_tiles = {}, {}, {}, {}, {}
 
-                v_banks = []
-                for half in range(GROUP // HALF):
-                    v = psum.tile([P, HALF, 2, HD], F32, tag="v", bufs=4)
-                    v_banks.append(v)
-                    for s in range(HALF):
-                        for qk in range(2):
-                            col = (half * HALF + s) * P
-                            nc.tensor.transpose(v[:, s, qk, :], v_t[:, qk, col : col + P], ident[:])
+        def load(g):
+            t, j0 = groups[g]
+            x_sb = stream.tile([P, GROUP, D], BF16, bufs=5)
+            nc.sync.dma_start(out=x_sb[:], in_=x_frames[t, :, j0 : j0 + GROUP, :])
+            x_tiles[g] = x_sb
 
-                sumsq = stream.tile([P, GROUP, 2], F32)
-                squares = stream.tile([P, GROUP, 2, HD], BF16, bufs=2)
-                for s in range(GROUP):
+        def transpose_x(g):
+            x_t_banks[g] = []
+            for half in range(HALVES):
+                x_t = psum.tile([P, 2, HALF * P], F32, tag="x_t", bufs=2)
+                x_t_banks[g].append(x_t)
+                for s in range(HALF):
+                    words = x_tiles[g][:, half * HALF + s, :].bitcast(F32)
+                    for u in range(2):
+                        nc.tensor.transpose(
+                            x_t[:, u, s * P : (s + 1) * P], words[:, u : D // 2 : 2], ident[:]
+                        )
+
+        def copy_x(g):
+            grouped = stream.tile([P, GROUP * P * 4], BF16, align_bytes=64)
+            grouped_tiles[g] = grouped
+            words = grouped[:].bitcast(F32).rearrange("p (h n u) -> p h n u", h=HALVES, u=2)
+            for half in range(HALVES):
+                nc.scalar.copy(
+                    out=words[:, half, :, :], in_=x_t_banks[g][half][:].rearrange("p u n -> p n u")
+                )
+
+        def quantise_x(g):
+            x_codes = stream.tile([P, GROUP * P], U32, align_bytes=64)
+            x_planes = stream.tile([P, GROUP * P], U8, align_bytes=64)
+            nc.vector.quantize_mx(
+                out=x_codes[:].bitcast(FP8X4), scales=x_planes[:], in_=grouped_tiles[g][:]
+            )
+            x_mx[g] = (x_codes, x_planes)
+
+        def project(g):
+            x_codes, x_planes = x_mx[g]
+            acc_banks[g] = []
+            for qk in range(2):
+                acc = psum.tile([P, GROUP * P], F32, tag="acc", bufs=2)
+                acc_banks[g].append(acc)
+                nc.tensor.matmul_mx(
+                    out=acc[:],
+                    lhsT=w_codes[:, qk, :].bitcast(FP8X4),
+                    lhsT_scale=w_planes[:, qk, :],
+                    rhs=x_codes[:].bitcast(FP8X4),
+                    rhs_scale=x_planes[:],
+                    start=True,
+                    stop=True,
+                )
+
+        def add_bias(g):
+            v_t = stream.tile([P, 2, GROUP * P], F32)
+            v_t_tiles[g] = v_t
+            for qk in range(2):
+                nc.scalar.activation(
+                    out=v_t[:, qk, :],
+                    in_=acc_banks[g][qk][:],
+                    func=ACT.Identity,
+                    bias=bias_col[:, qk : qk + 1],
+                )
+
+        def transpose_back(g):
+            v_banks[g] = []
+            for half in range(HALVES):
+                v = psum.tile([P, HALF, 2, HD], F32, tag="v", bufs=4)
+                v_banks[g].append(v)
+                for s in range(HALF):
+                    for qk in range(2):
+                        col = (half * HALF + s) * P
+                        nc.tensor.transpose(v[:, s, qk, :], v_t_tiles[g][:, qk, col : col + P], ident[:])
+
+        def norm(g):
+            sumsq = stream.tile([P, HALVES, HALF, 2], F32)
+            squares = stream.tile([P, HALVES, HALF, 2, HD], BF16, bufs=2)
+            for half in range(HALVES):
+                for s in range(HALF):
                     for qk in range(2):
                         nc.scalar.activation(
-                            out=squares[:, s, qk, :],
-                            in_=v_banks[s // HALF][:, s % HALF, qk, :],
+                            out=squares[:, half, s, qk, :],
+                            in_=v_banks[g][half][:, s, qk, :],
                             func=ACT.Square,
-                            accum_out=sumsq[:, s, qk : qk + 1],
+                            accum_out=sumsq[:, half, s, qk : qk + 1],
                         )
-                rms = stream.tile([P, GROUP, 2], F32)
-                nc.scalar.activation(
-                    out=rms[:], in_=sumsq[:], func=ACT.Sqrt, bias=eps_col[:, 0:1], scale=1.0 / HD
-                )
-                rstd = stream.tile([P, GROUP, 2], F32)
-                nc.vector.reciprocal(out=rstd[:], in_=rms[:])
+            rms = stream.tile([P, HALVES, HALF, 2], F32)
+            nc.scalar.activation(
+                out=rms[:], in_=sumsq[:], func=ACT.Sqrt, bias=eps_col[:, 0:1], scale=1.0 / HD
+            )
+            rms_tiles[g] = rms
 
-                products = stream.tile([P, 2, 2, GROUP, 2, PAIRS], F32)
-                for s in range(GROUP):
-                    for qk in range(2):
-                        v_pairs = v_banks[s // HALF][:, s % HALF, qk, :].rearrange(
-                            "p (pr two) -> p two pr", two=2
-                        )
-                        for src in range(2):
-                            nc.vector.scalar_tensor_tensor(
-                                out=products[:, src, qk, s, :, 0:PAIRS_T],
-                                in0=v_pairs[:, src, 0:PAIRS_T].unsqueeze(1).to_broadcast([P, 2, PAIRS_T]),
-                                scalar=rstd[:, s, qk : qk + 1],
-                                in1=table_t[:, t, qk, src, :, :],
-                                op0=ALU.mult,
-                                op1=ALU.mult,
-                            )
-                            nc.vector.scalar_tensor_tensor(
-                                out=products[:, src, qk, s, :, PAIRS_T:PAIRS],
-                                in0=v_pairs[:, src, PAIRS_T:PAIRS].unsqueeze(1).to_broadcast([P, 2, PAIRS_HW]),
-                                scalar=rstd[:, s, qk : qk + 1],
-                                in1=table_hw[:, j0 + s, qk, src, :, :],
-                                op0=ALU.mult,
-                                op1=ALU.mult,
-                            )
-
-                rotated = stream.tile([P, 2, GROUP, HD], F32)
+        def rotate_products(g, half):
+            t, j0 = groups[g]
+            if half == 0:
+                rstd = stream.tile([P, HALVES, HALF, 2], F32)
+                nc.vector.reciprocal(out=rstd[:], in_=rms_tiles[g][:])
+                rstd_tiles[g] = rstd
+                products = stream.tile([P, HALVES, 2, HALF, 2, HD], F32)
+                product_tiles[g] = products
+            products = product_tiles[g]
+            for s in range(HALF):
                 for qk in range(2):
-                    nc.gpsimd.tensor_tensor(
-                        out=rotated[:, qk, :, :].rearrange("p s (pr e) -> p s pr e", e=2),
-                        in0=products[:, 0, qk, :, :, :].rearrange("p s e pr -> p s pr e"),
-                        in1=products[:, 1, qk, :, :, :].rearrange("p s e pr -> p s pr e"),
-                        op=ALU.add,
+                    v = v_banks[g][half][:, s, qk, :]
+                    scale = rstd_tiles[g][:, half, s, qk : qk + 1]
+                    nc.vector.scalar_tensor_tensor(
+                        out=products[:, half, qk, s, :, 0:FEAT_T],
+                        in0=v[:, 0:FEAT_T].unsqueeze(1).to_broadcast([P, 2, FEAT_T]),
+                        scalar=scale,
+                        in1=table_t[:, t, qk, :, :],
+                        op0=ALU.mult,
+                        op1=ALU.mult,
                     )
-                    nc.sync.dma_start(
-                        out=out_frames[qk][t, :, j0 : j0 + GROUP, :], in_=rotated[:, qk, :, :]
+                    nc.vector.scalar_tensor_tensor(
+                        out=products[:, half, qk, s, :, FEAT_T:HD],
+                        in0=v[:, FEAT_T:HD].unsqueeze(1).to_broadcast([P, 2, HD - FEAT_T]),
+                        scalar=scale,
+                        in1=table_hw[:, j0 + half * HALF + s, qk, :, :],
+                        op0=ALU.mult,
+                        op1=ALU.mult,
                     )
+
+        def rotate_add(g):
+            rotated = stream.tile([P, 2, HALVES, HALF, HD], F32)
+            rotated_tiles[g] = rotated
+            for half in range(HALVES):
+                terms = product_tiles[g][:, half, :, :, :, :].rearrange(
+                    "p q s e (pr two) -> p two q s pr e", two=2
+                )
+                nc.gpsimd.tensor_tensor(
+                    out=rotated[:, :, half, :, :].rearrange("p q s (pr e) -> p q s pr e", e=2),
+                    in0=terms[:, 0],
+                    in1=terms[:, 1],
+                    op=ALU.add,
+                )
+
+        def store(g):
+            t, j0 = groups[g]
+            for qk in range(2):
+                nc.sync.dma_start(
+                    out=out_frames[qk][t, :, j0 : j0 + GROUP, :],
+                    in_=rotated_tiles[g][:, qk, :, :, :].rearrange("p h s f -> p (h s) f"),
+                )
+
+        def when(g, stage, *args):
+            if 0 <= g < n_groups:
+                stage(g, *args)
+
+        with tc.manual_schedule():
+            for g in range(LOADS_AHEAD):
+                load(g)
+            transpose_x(0)
+            for step in range(n_groups + 4):
+                when(step + LOADS_AHEAD, load)
+                when(step, copy_x)
+                when(step + 1, transpose_x)
+                when(step - 3, rotate_products, 0)
+                when(step, quantise_x)
+                if step < 2:
+                    build_tables(step)
+                when(step - 1, add_bias)
+                when(step, project)
+                when(step - 2, norm)
+                when(step - 3, rotate_products, 1)
+                when(step - 1, transpose_back)
+                when(step - 3, rotate_add)
+                when(step - 3, store)

@@ -141,7 +141,7 @@ def tile_multiheadattention_pa_t_kernel(
         groups = [(t, j0) for t in range(FRAMES) for j0 in range(0, SLOTS, GROUP)]
         n_groups = len(groups)
         x_tiles, x_t_banks, grouped_tiles, x_mx, acc_banks, v_t_tiles = {}, {}, {}, {}, {}, {}
-        v_banks, rms_tiles, rstd_tiles, product_tiles, rotated_tiles = {}, {}, {}, {}, {}
+        v_banks, sumsq_tiles, rstd_tiles, product_tiles, rotated_tiles = {}, {}, {}, {}, {}
 
         def load(g):
             t, j0 = groups[g]
@@ -166,9 +166,8 @@ def tile_multiheadattention_pa_t_kernel(
             grouped_tiles[g] = grouped
             words = grouped[:].bitcast(F32).rearrange("p (h n u) -> p h n u", h=HALVES, u=2)
             for half in range(HALVES):
-                nc.scalar.copy(
-                    out=words[:, half, :, :], in_=x_t_banks[g][half][:].rearrange("p u n -> p n u")
-                )
+                copy = nc.vector.tensor_copy if (g % 2 == 1 and half == 1) else nc.scalar.copy
+                copy(out=words[:, half, :, :], in_=x_t_banks[g][half][:].rearrange("p u n -> p n u"))
 
         def quantise_x(g):
             x_codes = stream.tile([P, GROUP * P], U32, align_bytes=64)
@@ -227,18 +226,22 @@ def tile_multiheadattention_pa_t_kernel(
                             func=ACT.Square,
                             accum_out=sumsq[:, half, s, qk : qk + 1],
                         )
-            rms = stream.tile([P, HALVES, HALF, 2], F32)
+            sumsq_tiles[g] = sumsq
+
+        def inverse_rms(g):
+            rstd = stream.tile([P, HALVES, HALF, 2], F32)
             nc.scalar.activation(
-                out=rms[:], in_=sumsq[:], func=ACT.Sqrt, bias=eps_col[:, 0:1], scale=1.0 / HD
+                out=rstd[:],
+                in_=sumsq_tiles[g][:],
+                func=ACT.Abs_reciprocal_sqrt,
+                bias=eps_col[:, 0:1],
+                scale=1.0 / HD,
             )
-            rms_tiles[g] = rms
+            rstd_tiles[g] = rstd
 
         def rotate_products(g, half):
             t, j0 = groups[g]
             if half == 0:
-                rstd = stream.tile([P, HALVES, HALF, 2], F32)
-                nc.vector.reciprocal(out=rstd[:], in_=rms_tiles[g][:])
-                rstd_tiles[g] = rstd
                 products = stream.tile([P, HALVES, 2, HALF, 2, HD], F32)
                 product_tiles[g] = products
             products = product_tiles[g]
@@ -296,6 +299,7 @@ def tile_multiheadattention_pa_t_kernel(
             for step in range(n_groups + 4):
                 when(step + LOADS_AHEAD, load)
                 when(step, copy_x)
+                when(step - 3, inverse_rms)
                 when(step + 1, transpose_x)
                 when(step - 3, rotate_products, 0)
                 when(step, quantise_x)

@@ -79,6 +79,8 @@ def tile_multiheadattention_pa_t_kernel(
 
         eps_col = consts.tile([P, 1], F32)
         nc.vector.memset(eps_col[:], EPS)
+        table_warm_up = consts.tile([P, 1], F32)
+        nc.scalar.activation(out=table_warm_up[:], in_=eps_col[:], func=ACT.Abs_reciprocal_sqrt)
 
         gains = consts.tile([P, 2, HD], BF16)
         nc.scalar.dma_start(out=gains[:, 0, :], in_=q_scale.partition_broadcast(P))
@@ -119,19 +121,19 @@ def tile_multiheadattention_pa_t_kernel(
         def build_tables(qk):
             for e, (turn_t, turn_h, turn_w) in enumerate(((cs_t, cs_h, cs_w), (sc_t, sc_h, sc_w))):
                 gain = signed_gains[:, e, qk, :, :].rearrange("p pr two -> p (pr two)")
-                nc.vector.tensor_tensor(
+                nc.gpsimd.tensor_tensor(
                     out=table_t[:, :, qk, e, :],
                     in0=turn_t[:].rearrange("p (t a) b -> p t (a b)", t=FRAMES),
                     in1=gain[:, 0:FEAT_T].unsqueeze(1).to_broadcast([P, FRAMES, FEAT_T]),
                     op=ALU.mult,
                 )
-                nc.vector.tensor_tensor(
+                nc.gpsimd.tensor_tensor(
                     out=table_hw[:, :, qk, e, 0:FEAT_H],
                     in0=turn_h[:].rearrange("p a b -> p (a b)").unsqueeze(1).to_broadcast([P, SLOTS, FEAT_H]),
                     in1=gain[:, FEAT_T : FEAT_T + FEAT_H].unsqueeze(1).to_broadcast([P, SLOTS, FEAT_H]),
                     op=ALU.mult,
                 )
-                nc.vector.tensor_tensor(
+                nc.gpsimd.tensor_tensor(
                     out=table_hw[:, :, qk, e, FEAT_H : FEAT_H + FEAT_W],
                     in0=turn_w[:].rearrange("p (j a) b -> p j (a b)", j=SLOTS),
                     in1=gain[:, FEAT_T + FEAT_H : HD].unsqueeze(1).to_broadcast([P, SLOTS, FEAT_W]),
@@ -146,7 +148,9 @@ def tile_multiheadattention_pa_t_kernel(
         def load(g):
             t, j0 = groups[g]
             x_sb = stream.tile([P, GROUP, D], BF16, bufs=5)
-            nc.sync.dma_start(out=x_sb[:], in_=x_frames[t, :, j0 : j0 + GROUP, :])
+            for half in range(HALVES):
+                slots = slice(half * HALF, (half + 1) * HALF)
+                nc.sync.dma_start(out=x_sb[:, slots, :], in_=x_frames[t, :, j0:, :][:, slots, :])
             x_tiles[g] = x_sb
 
         def transpose_x(g):
@@ -292,6 +296,9 @@ def tile_multiheadattention_pa_t_kernel(
             if 0 <= g < n_groups:
                 stage(g, *args)
 
+        for qk in range(2):
+            build_tables(qk)
+
         with tc.manual_schedule():
             for g in range(LOADS_AHEAD):
                 load(g)
@@ -303,8 +310,6 @@ def tile_multiheadattention_pa_t_kernel(
                 when(step + 1, transpose_x)
                 when(step - 3, rotate_products, 0)
                 when(step, quantise_x)
-                if step < 2:
-                    build_tables(step)
                 when(step - 1, add_bias)
                 when(step, project)
                 when(step - 2, norm)

@@ -49,6 +49,20 @@ def tile_multiheadattention_pa_t_kernel(
         stream = ctx.enter_context(tc.tile_pool(name="stream", bufs=3))
         psum = ctx.enter_context(tc.psum_pool(name="psum", bufs=2))
 
+        groups = [(t, j0) for t in range(FRAMES) for j0 in range(0, SLOTS, GROUP)]
+        n_groups = len(groups)
+        x_tiles = {}
+
+        def load(g):
+            t, j0 = groups[g]
+            x_sb = stream.tile([P, GROUP, D], BF16, bufs=5)
+            for half in range(HALVES):
+                slots = slice(half * HALF, (half + 1) * HALF)
+                nc.sync.dma_start(out=x_sb[:, slots, :], in_=x_frames[t, :, j0:, :][:, slots, :])
+            x_tiles[g] = x_sb
+
+        load(0)
+
         w_codes = consts.tile([P, 2, HD], U32, align_bytes=64)
         w_planes = consts.tile([P, 2, HD], U8, align_bytes=64)
         nc.vector.memset(w_planes[:].rearrange("p a n -> p (a n)").bitcast(I32), 0)
@@ -62,6 +76,9 @@ def tile_multiheadattention_pa_t_kernel(
                     out=w_planes[32 * quad : 32 * quad + 4, qk, :].bitcast(I32),
                     in_=scales[0, 4 * quad : 4 * quad + 4, :].bitcast(I32),
                 )
+
+        for g in range(1, LOADS_AHEAD):
+            load(g)
 
         ident = consts.tile([P, P], F32)
         make_identity(nc, ident[:])
@@ -140,18 +157,8 @@ def tile_multiheadattention_pa_t_kernel(
                     op=ALU.mult,
                 )
 
-        groups = [(t, j0) for t in range(FRAMES) for j0 in range(0, SLOTS, GROUP)]
-        n_groups = len(groups)
-        x_tiles, x_t_banks, grouped_tiles, x_mx, acc_banks, v_t_tiles = {}, {}, {}, {}, {}, {}
+        x_t_banks, grouped_tiles, x_mx, acc_banks, v_t_tiles = {}, {}, {}, {}, {}
         v_banks, sumsq_tiles, rstd_tiles, product_tiles, rotated_tiles = {}, {}, {}, {}, {}
-
-        def load(g):
-            t, j0 = groups[g]
-            x_sb = stream.tile([P, GROUP, D], BF16, bufs=5)
-            for half in range(HALVES):
-                slots = slice(half * HALF, (half + 1) * HALF)
-                nc.sync.dma_start(out=x_sb[:, slots, :], in_=x_frames[t, :, j0:, :][:, slots, :])
-            x_tiles[g] = x_sb
 
         def transpose_x(g):
             x_t_banks[g] = []
@@ -300,8 +307,6 @@ def tile_multiheadattention_pa_t_kernel(
             build_tables(qk)
 
         with tc.manual_schedule():
-            for g in range(LOADS_AHEAD):
-                load(g)
             transpose_x(0)
             for step in range(n_groups + 4):
                 when(step + LOADS_AHEAD, load)

@@ -83,22 +83,8 @@ def tile_multiheadattention_pa_t_kernel(
         ident = consts.tile([P, P], F32)
         make_identity(nc, ident[:])
 
-        bias_rows = consts.tile([P, HD], BF16)
-        nc.vector.memset(bias_rows[:], 0.0)
-        nc.scalar.dma_start(out=bias_rows[0:1, :], in_=bq.unsqueeze(0))
-        nc.scalar.dma_start(out=bias_rows[1:2, :], in_=bk.unsqueeze(0))
-        bias_rows_f32 = consts.tile([P, HD], F32)
-        nc.vector.tensor_copy(out=bias_rows_f32[:], in_=bias_rows[:])
-        bias_ps = psum.tile([P, HALF, 2, HD], F32, tag="v", bufs=4)
-        nc.tensor.transpose(bias_ps[:, 0, 0, :], bias_rows_f32[:], ident[:])
-        bias_col = consts.tile([P, 2], F32)
-        nc.vector.tensor_copy(out=bias_col[:], in_=bias_ps[:, 0, 0, 0:2])
-
         eps_col = consts.tile([P, 1], F32)
         nc.vector.memset(eps_col[:], EPS)
-        table_warm_up = consts.tile([P, 1], F32)
-        nc.scalar.activation(out=table_warm_up[:], in_=eps_col[:], func=ACT.Abs_reciprocal_sqrt)
-
         gains = consts.tile([P, 2, HD], BF16)
         nc.scalar.dma_start(out=gains[:, 0, :], in_=q_scale.partition_broadcast(P))
         nc.scalar.dma_start(out=gains[:, 1, :], in_=k_scale.partition_broadcast(P))
@@ -120,6 +106,22 @@ def tile_multiheadattention_pa_t_kernel(
             .to_broadcast([32, 4, SLOTS * 2 * PAIRS_W]),
         )
 
+        bias_rows = consts.tile([P, HD], BF16)
+        nc.vector.memset(bias_rows[:], 0.0)
+        nc.scalar.dma_start(out=bias_rows[0:1, :], in_=bq.unsqueeze(0))
+        nc.scalar.dma_start(out=bias_rows[1:2, :], in_=bk.unsqueeze(0))
+        bias_rows_f32 = consts.tile([P, HD], F32)
+        nc.vector.tensor_copy(out=bias_rows_f32[:], in_=bias_rows[:])
+        bias_col = consts.tile([P, 2], F32)
+
+        def transpose_bias():
+            bias_ps = psum.tile([P, HALF, 2, HD], F32, tag="v", bufs=4)
+            nc.tensor.transpose(bias_ps[:, 0, 0, :], bias_rows_f32[:], ident[:])
+            nc.vector.tensor_copy(out=bias_col[:], in_=bias_ps[:, 0, 0, 0:2])
+
+        table_warm_up = consts.tile([P, 1], F32)
+        nc.scalar.activation(out=table_warm_up[:], in_=eps_col[:], func=ACT.Abs_reciprocal_sqrt)
+
         sc_t = consts.tile([P, FRAMES * PAIRS_T, 2], BF16)
         sc_h = consts.tile([P, PAIRS_H, 2], BF16)
         sc_w = consts.tile([P, SLOTS * PAIRS_W, 2], BF16)
@@ -135,22 +137,22 @@ def tile_multiheadattention_pa_t_kernel(
         table_t = consts.tile([P, FRAMES, 2, 2, 2 * PAIRS_T], F32)
         table_hw = consts.tile([P, SLOTS, 2, 2, 2 * PAIRS_HW], F32)
 
-        def build_tables(qk):
+        for qk, engine in ((0, nc.vector), (1, nc.gpsimd)):
             for e, (turn_t, turn_h, turn_w) in enumerate(((cs_t, cs_h, cs_w), (sc_t, sc_h, sc_w))):
                 gain = signed_gains[:, e, qk, :, :].rearrange("p pr two -> p (pr two)")
-                nc.gpsimd.tensor_tensor(
+                engine.tensor_tensor(
                     out=table_t[:, :, qk, e, :],
                     in0=turn_t[:].rearrange("p (t a) b -> p t (a b)", t=FRAMES),
                     in1=gain[:, 0:FEAT_T].unsqueeze(1).to_broadcast([P, FRAMES, FEAT_T]),
                     op=ALU.mult,
                 )
-                nc.gpsimd.tensor_tensor(
+                engine.tensor_tensor(
                     out=table_hw[:, :, qk, e, 0:FEAT_H],
                     in0=turn_h[:].rearrange("p a b -> p (a b)").unsqueeze(1).to_broadcast([P, SLOTS, FEAT_H]),
                     in1=gain[:, FEAT_T : FEAT_T + FEAT_H].unsqueeze(1).to_broadcast([P, SLOTS, FEAT_H]),
                     op=ALU.mult,
                 )
-                nc.gpsimd.tensor_tensor(
+                engine.tensor_tensor(
                     out=table_hw[:, :, qk, e, FEAT_H : FEAT_H + FEAT_W],
                     in0=turn_w[:].rearrange("p (j a) b -> p j (a b)", j=SLOTS),
                     in1=gain[:, FEAT_T + FEAT_H : HD].unsqueeze(1).to_broadcast([P, SLOTS, FEAT_W]),
@@ -303,11 +305,9 @@ def tile_multiheadattention_pa_t_kernel(
             if 0 <= g < n_groups:
                 stage(g, *args)
 
-        for qk in range(2):
-            build_tables(qk)
-
         with tc.manual_schedule():
             transpose_x(0)
+            transpose_bias()
             for step in range(n_groups + 4):
                 when(step + LOADS_AHEAD, load)
                 when(step, copy_x)

@@ -227,9 +227,12 @@ def tile_multiheadattention_pa_t_kernel(
                         col = (half * HALF + s) * P
                         nc.tensor.transpose(v[:, s, qk, :], v_t_tiles[g][:, qk, col : col + P], ident[:])
 
+        last = n_groups - 1
+
         def norm(g):
-            sumsq = stream.tile([P, HALVES, HALF, 2], F32)
             squares = stream.tile([P, HALVES, HALF, 2, HD], BF16, bufs=2)
+            sumsq = stream.tile([P, HALVES, HALF, 2], F32)
+            sumsq_tiles[g] = sumsq
             for half in range(HALVES):
                 for s in range(HALF):
                     for qk in range(2):
@@ -239,31 +242,39 @@ def tile_multiheadattention_pa_t_kernel(
                             func=ACT.Square,
                             accum_out=sumsq[:, half, s, qk : qk + 1],
                         )
-            sumsq_tiles[g] = sumsq
+                if g == last:
+                    inverse_rms_of(g, half, sumsq[:, half, :, :])
+
+        def inverse_rms_of(g, half, sums):
+            rstd = stream.tile([P, HALVES, HALF, 2], F32)
+            out = rstd[:] if half is None else rstd[:, half, :, :]
+            nc.scalar.activation(
+                out=out, in_=sums, func=ACT.Abs_reciprocal_sqrt, bias=eps_col[:, 0:1], scale=1.0 / HD
+            )
+            for h in range(HALVES) if half is None else [half]:
+                rstd_tiles[g, h] = rstd
 
         def inverse_rms(g):
-            rstd = stream.tile([P, HALVES, HALF, 2], F32)
-            nc.scalar.activation(
-                out=rstd[:],
-                in_=sumsq_tiles[g][:],
-                func=ACT.Abs_reciprocal_sqrt,
-                bias=eps_col[:, 0:1],
-                scale=1.0 / HD,
-            )
-            rstd_tiles[g] = rstd
+            if g != last:
+                inverse_rms_of(g, None, sumsq_tiles[g][:])
 
         def rotate_products(g, half):
             t, j0 = groups[g]
-            if half == 0:
-                products = stream.tile([P, HALVES, 2, HALF, 2, HD], F32)
-                product_tiles[g] = products
-            products = product_tiles[g]
+            if g == last:
+                products = stream.tile([P, 2, HALF, 2, HD], F32, name="half_products", bufs=2)
+                product_tiles[g, half] = products
+            elif half == 0:
+                products = stream.tile([P, 2, GROUP, 2, HD], F32)
+                for h in range(HALVES):
+                    product_tiles[g, h] = products
+            products = product_tiles[g, half]
             for s in range(HALF):
                 for qk in range(2):
+                    slot = s if g == last else half * HALF + s
                     v = v_banks[g][half][:, s, qk, :]
-                    scale = rstd_tiles[g][:, half, s, qk : qk + 1]
+                    scale = rstd_tiles[g, half][:, half, s, qk : qk + 1]
                     nc.vector.scalar_tensor_tensor(
-                        out=products[:, half, qk, s, :, 0:FEAT_T],
+                        out=products[:, qk, slot, :, 0:FEAT_T],
                         in0=v[:, 0:FEAT_T].unsqueeze(1).to_broadcast([P, 2, FEAT_T]),
                         scalar=scale,
                         in1=table_t[:, t, qk, :, :],
@@ -271,7 +282,7 @@ def tile_multiheadattention_pa_t_kernel(
                         op1=ALU.mult,
                     )
                     nc.vector.scalar_tensor_tensor(
-                        out=products[:, half, qk, s, :, FEAT_T:HD],
+                        out=products[:, qk, slot, :, FEAT_T:HD],
                         in0=v[:, FEAT_T:HD].unsqueeze(1).to_broadcast([P, 2, HD - FEAT_T]),
                         scalar=scale,
                         in1=table_hw[:, j0 + half * HALF + s, qk, :, :],
@@ -280,26 +291,25 @@ def tile_multiheadattention_pa_t_kernel(
                     )
 
         def rotate_add(g):
-            rotated = stream.tile([P, 2, HALVES, HALF, HD], F32)
+            rotated = stream.tile([P, 2, GROUP, HD], F32)
             rotated_tiles[g] = rotated
+            sums = rotated[:].rearrange("p q s (pr e) -> p q s pr e", e=2)
+            if g != last:
+                terms = product_tiles[g, 0][:].rearrange("p q s e (pr two) -> p two q s pr e", two=2)
+                nc.gpsimd.tensor_tensor(out=sums, in0=terms[:, 0], in1=terms[:, 1], op=ALU.add)
+                return
             for half in range(HALVES):
-                terms = product_tiles[g][:, half, :, :, :, :].rearrange(
-                    "p q s e (pr two) -> p two q s pr e", two=2
-                )
-                nc.gpsimd.tensor_tensor(
-                    out=rotated[:, :, half, :, :].rearrange("p q s (pr e) -> p q s pr e", e=2),
-                    in0=terms[:, 0],
-                    in1=terms[:, 1],
-                    op=ALU.add,
-                )
+                terms = product_tiles[g, half][:].rearrange("p q s e (pr two) -> p two q s pr e", two=2)
+                slots = slice(half * HALF, (half + 1) * HALF)
+                for qk in range(2):
+                    nc.vector.tensor_tensor(
+                        out=sums[:, qk, slots], in0=terms[:, 0, qk], in1=terms[:, 1, qk], op=ALU.add
+                    )
 
         def store(g):
             t, j0 = groups[g]
             for qk in range(2):
-                nc.sync.dma_start(
-                    out=out_frames[qk][t, :, j0 : j0 + GROUP, :],
-                    in_=rotated_tiles[g][:, qk, :, :, :].rearrange("p h s f -> p (h s) f"),
-                )
+                nc.sync.dma_start(out=out_frames[qk][t, :, j0 : j0 + GROUP, :], in_=rotated_tiles[g][:, qk, :, :])
 
         def when(g, stage, *args):
             if 0 <= g < n_groups:

@@ -260,21 +260,15 @@ def tile_multiheadattention_pa_t_kernel(
 
         def rotate_products(g, half):
             t, j0 = groups[g]
-            if g == last:
-                products = stream.tile([P, 2, HALF, 2, HD], F32, name="half_products", bufs=2)
-                product_tiles[g, half] = products
-            elif half == 0:
-                products = stream.tile([P, 2, GROUP, 2, HD], F32)
-                for h in range(HALVES):
-                    product_tiles[g, h] = products
-            products = product_tiles[g, half]
             for s in range(HALF):
+                slot = half * HALF + s
+                products = stream.tile([P, 2, 2, HD], F32, bufs=3 * GROUP)
+                product_tiles[g, slot] = products
                 for qk in range(2):
-                    slot = s if g == last else half * HALF + s
                     v = v_banks[g][half][:, s, qk, :]
                     scale = rstd_tiles[g, half][:, half, s, qk : qk + 1]
                     nc.vector.scalar_tensor_tensor(
-                        out=products[:, qk, slot, :, 0:FEAT_T],
+                        out=products[:, qk, :, 0:FEAT_T],
                         in0=v[:, 0:FEAT_T].unsqueeze(1).to_broadcast([P, 2, FEAT_T]),
                         scalar=scale,
                         in1=table_t[:, t, qk, :, :],
@@ -282,10 +276,10 @@ def tile_multiheadattention_pa_t_kernel(
                         op1=ALU.mult,
                     )
                     nc.vector.scalar_tensor_tensor(
-                        out=products[:, qk, slot, :, FEAT_T:HD],
+                        out=products[:, qk, :, FEAT_T:HD],
                         in0=v[:, FEAT_T:HD].unsqueeze(1).to_broadcast([P, 2, HD - FEAT_T]),
                         scalar=scale,
-                        in1=table_hw[:, j0 + half * HALF + s, qk, :, :],
+                        in1=table_hw[:, j0 + slot, qk, :, :],
                         op0=ALU.mult,
                         op1=ALU.mult,
                     )
@@ -294,17 +288,10 @@ def tile_multiheadattention_pa_t_kernel(
             rotated = stream.tile([P, 2, GROUP, HD], F32)
             rotated_tiles[g] = rotated
             sums = rotated[:].rearrange("p q s (pr e) -> p q s pr e", e=2)
-            if g != last:
-                terms = product_tiles[g, 0][:].rearrange("p q s e (pr two) -> p two q s pr e", two=2)
-                nc.gpsimd.tensor_tensor(out=sums, in0=terms[:, 0], in1=terms[:, 1], op=ALU.add)
-                return
-            for half in range(HALVES):
-                terms = product_tiles[g, half][:].rearrange("p q s e (pr two) -> p two q s pr e", two=2)
-                slots = slice(half * HALF, (half + 1) * HALF)
-                for qk in range(2):
-                    nc.vector.tensor_tensor(
-                        out=sums[:, qk, slots], in0=terms[:, 0, qk], in1=terms[:, 1, qk], op=ALU.add
-                    )
+            engine = nc.vector if g == last else nc.gpsimd
+            for slot in range(GROUP):
+                terms = product_tiles[g, slot][:].rearrange("p q e (pr two) -> p two q pr e", two=2)
+                engine.tensor_tensor(out=sums[:, :, slot], in0=terms[:, 0], in1=terms[:, 1], op=ALU.add)
 
         def store(g):
             t, j0 = groups[g]

@@ -260,15 +260,14 @@ def tile_multiheadattention_pa_t_kernel(
 
         def rotate_products(g, half):
             t, j0 = groups[g]
+            products = stream.tile([P, 2, HALF, 2, HD], F32, bufs=3 * HALVES)
+            product_tiles[g, half] = products
             for s in range(HALF):
-                slot = half * HALF + s
-                products = stream.tile([P, 2, 2, HD], F32, bufs=3 * GROUP)
-                product_tiles[g, slot] = products
                 for qk in range(2):
                     v = v_banks[g][half][:, s, qk, :]
                     scale = rstd_tiles[g, half][:, half, s, qk : qk + 1]
                     nc.vector.scalar_tensor_tensor(
-                        out=products[:, qk, :, 0:FEAT_T],
+                        out=products[:, qk, s, :, 0:FEAT_T],
                         in0=v[:, 0:FEAT_T].unsqueeze(1).to_broadcast([P, 2, FEAT_T]),
                         scalar=scale,
                         in1=table_t[:, t, qk, :, :],
@@ -276,10 +275,10 @@ def tile_multiheadattention_pa_t_kernel(
                         op1=ALU.mult,
                     )
                     nc.vector.scalar_tensor_tensor(
-                        out=products[:, qk, :, FEAT_T:HD],
+                        out=products[:, qk, s, :, FEAT_T:HD],
                         in0=v[:, FEAT_T:HD].unsqueeze(1).to_broadcast([P, 2, HD - FEAT_T]),
                         scalar=scale,
-                        in1=table_hw[:, j0 + slot, qk, :, :],
+                        in1=table_hw[:, j0 + half * HALF + s, qk, :, :],
                         op0=ALU.mult,
                         op1=ALU.mult,
                     )
@@ -288,10 +287,16 @@ def tile_multiheadattention_pa_t_kernel(
             rotated = stream.tile([P, 2, GROUP, HD], F32)
             rotated_tiles[g] = rotated
             sums = rotated[:].rearrange("p q s (pr e) -> p q s pr e", e=2)
-            engine = nc.vector if g == last else nc.gpsimd
-            for slot in range(GROUP):
-                terms = product_tiles[g, slot][:].rearrange("p q e (pr two) -> p two q pr e", two=2)
-                engine.tensor_tensor(out=sums[:, :, slot], in0=terms[:, 0], in1=terms[:, 1], op=ALU.add)
+            for half in range(HALVES):
+                terms = product_tiles[g, half][:].rearrange("p q s e (pr two) -> p two q s pr e", two=2)
+                slots = slice(half * HALF, (half + 1) * HALF)
+                if g != last:
+                    nc.gpsimd.tensor_tensor(out=sums[:, :, slots], in0=terms[:, 0], in1=terms[:, 1], op=ALU.add)
+                    continue
+                for qk in range(2):
+                    nc.vector.tensor_tensor(
+                        out=sums[:, qk, slots], in0=terms[:, 0, qk], in1=terms[:, 1, qk], op=ALU.add
+                    )
 
         def store(g):
             t, j0 = groups[g]

@@ -125,39 +125,53 @@ def tile_multiheadattention_pa_t_kernel(
         sc_t = consts.tile([P, FRAMES * PAIRS_T, 2], BF16)
         sc_h = consts.tile([P, PAIRS_H, 2], BF16)
         sc_w = consts.tile([P, SLOTS * PAIRS_W, 2], BF16)
-        for swapped, given in ((sc_t, cs_t), (sc_h, cs_h), (sc_w, cs_w)):
-            for i in range(2):
-                nc.vector.tensor_copy(out=swapped[:, :, i], in_=given[:, :, 1 - i])
         signed_gains = consts.tile([P, 2, 2, PAIRS, 2], F32)
-        gain_pairs = gains[:].rearrange("p q (pr two) -> p q pr two", two=2)
-        nc.vector.tensor_copy(out=signed_gains[:, 0, :, :, 0], in_=gain_pairs[:, :, :, 0])
-        nc.vector.tensor_scalar_mul(out=signed_gains[:, 0, :, :, 1], in0=gain_pairs[:, :, :, 1], scalar1=-1.0)
-        nc.vector.tensor_copy(out=signed_gains[:, 1, :, :, :], in_=gain_pairs)
-
         table_t = consts.tile([P, FRAMES, 2, 2, 2 * PAIRS_T], F32)
         table_hw = consts.tile([P, SLOTS, 2, 2, 2 * PAIRS_HW], F32)
 
-        for qk, engine in ((0, nc.vector), (1, nc.gpsimd)):
-            for e, (turn_t, turn_h, turn_w) in enumerate(((cs_t, cs_h, cs_w), (sc_t, sc_h, sc_w))):
-                gain = signed_gains[:, e, qk, :, :].rearrange("p pr two -> p (pr two)")
+        def prepare_tables():
+            for swapped, given in ((sc_t, cs_t), (sc_h, cs_h), (sc_w, cs_w)):
+                for i in range(2):
+                    nc.vector.tensor_copy(out=swapped[:, :, i], in_=given[:, :, 1 - i])
+            gain_pairs = gains[:].rearrange("p q (pr two) -> p q pr two", two=2)
+            nc.vector.tensor_copy(out=signed_gains[:, 0, :, :, 0], in_=gain_pairs[:, :, :, 0])
+            nc.vector.tensor_scalar_mul(out=signed_gains[:, 0, :, :, 1], in0=gain_pairs[:, :, :, 1], scalar1=-1.0)
+            nc.vector.tensor_copy(out=signed_gains[:, 1, :, :, :], in_=gain_pairs)
+
+        def build_table(engine, qk, e, part):
+            turn_t, turn_h, turn_w = ((cs_t, cs_h, cs_w), (sc_t, sc_h, sc_w))[e]
+            gain = signed_gains[:, e, qk, :, :].rearrange("p pr two -> p (pr two)")
+            if part == 0:
                 engine.tensor_tensor(
                     out=table_t[:, :, qk, e, :],
                     in0=turn_t[:].rearrange("p (t a) b -> p t (a b)", t=FRAMES),
                     in1=gain[:, 0:FEAT_T].unsqueeze(1).to_broadcast([P, FRAMES, FEAT_T]),
                     op=ALU.mult,
                 )
+            elif part == 1:
                 engine.tensor_tensor(
                     out=table_hw[:, :, qk, e, 0:FEAT_H],
                     in0=turn_h[:].rearrange("p a b -> p (a b)").unsqueeze(1).to_broadcast([P, SLOTS, FEAT_H]),
                     in1=gain[:, FEAT_T : FEAT_T + FEAT_H].unsqueeze(1).to_broadcast([P, SLOTS, FEAT_H]),
                     op=ALU.mult,
                 )
+            else:
                 engine.tensor_tensor(
                     out=table_hw[:, :, qk, e, FEAT_H : FEAT_H + FEAT_W],
                     in0=turn_w[:].rearrange("p (j a) b -> p j (a b)", j=SLOTS),
                     in1=gain[:, FEAT_T + FEAT_H : HD].unsqueeze(1).to_broadcast([P, SLOTS, FEAT_W]),
                     op=ALU.mult,
                 )
+
+        prepare_tables()
+        for e in range(2):
+            for part in (1, 2):
+                build_table(nc.gpsimd, 1, e, part)
+        vector_pieces = [(0, e, part) for part in (1, 2, 0) for e in range(2)] + [(1, e, 0) for e in range(2)]
+
+        def tables_behind_quantise(step):
+            for qk, e, part in vector_pieces[3 * step - (step > 0) : 3 * step + 2]:
+                build_table(nc.vector, qk, e, part)
 
         x_t_banks, grouped_tiles, x_mx, acc_banks, v_t_tiles = {}, {}, {}, {}, {}
         v_banks, sumsq_tiles, rstd_tiles, product_tiles, rotated_tiles = {}, {}, {}, {}, {}
@@ -317,6 +331,8 @@ def tile_multiheadattention_pa_t_kernel(
                 when(step + 1, transpose_x)
                 when(step - 3, rotate_products, 0)
                 when(step, quantise_x)
+                if step < 3:
+                    tables_behind_quantise(step)
                 when(step - 1, add_bias)
                 when(step, project)
                 when(step - 2, norm)

@@ -25,10 +25,8 @@ LOADS_AHEAD = 3
 PAIRS_T = 22
 PAIRS_H = 21
 PAIRS_W = 21
-PAIRS_HW = PAIRS_H + PAIRS_W
-FEAT_T = 2 * PAIRS_T
-FEAT_H = 2 * PAIRS_H
-FEAT_W = 2 * PAIRS_W
+HALF_HD = HD // 2
+PAIRS_H0 = PAIRS // 2 - PAIRS_T
 EPS = 1e-6
 
 FLOPS = 2 * 8192 * D * 2 * HD
@@ -122,56 +120,53 @@ def tile_multiheadattention_pa_t_kernel(
         table_warm_up = consts.tile([P, 1], F32)
         nc.scalar.activation(out=table_warm_up[:], in_=eps_col[:], func=ACT.Abs_reciprocal_sqrt)
 
-        sc_t = consts.tile([P, FRAMES * PAIRS_T, 2], BF16)
-        sc_h = consts.tile([P, PAIRS_H, 2], BF16)
-        sc_w = consts.tile([P, SLOTS * PAIRS_W, 2], BF16)
-        signed_gains = consts.tile([P, 2, 2, PAIRS, 2], F32)
-        table_t = consts.tile([P, FRAMES, 2, 2, 2 * PAIRS_T], F32)
-        table_hw = consts.tile([P, SLOTS, 2, 2, 2 * PAIRS_HW], F32)
+        turns_t = consts.tile([P, FRAMES * PAIRS_T, 2, 2], BF16)
+        turns_h = consts.tile([P, PAIRS_H, 2, 2], BF16)
+        turns_w = consts.tile([P, SLOTS * PAIRS_W, 2, 2], BF16)
+        signed_gains = consts.tile([P, 2, PAIRS, 2, 2], F32)
+        tables = consts.tile([P, FRAMES + SLOTS, 2, HALF_HD, 2], F32)
 
         def prepare_tables():
-            for swapped, given in ((sc_t, cs_t), (sc_h, cs_h), (sc_w, cs_w)):
-                for i in range(2):
-                    nc.vector.tensor_copy(out=swapped[:, :, i], in_=given[:, :, 1 - i])
+            for turns, given in ((turns_t, cs_t), (turns_h, cs_h), (turns_w, cs_w)):
+                nc.vector.tensor_copy(out=turns[:, :, 0, :], in_=given[:])
+                for e in range(2):
+                    nc.vector.tensor_copy(out=turns[:, :, 1, e], in_=given[:, :, 1 - e])
             gain_pairs = gains[:].rearrange("p q (pr two) -> p q pr two", two=2)
-            nc.vector.tensor_copy(out=signed_gains[:, 0, :, :, 0], in_=gain_pairs[:, :, :, 0])
-            nc.vector.tensor_scalar_mul(out=signed_gains[:, 0, :, :, 1], in0=gain_pairs[:, :, :, 1], scalar1=-1.0)
-            nc.vector.tensor_copy(out=signed_gains[:, 1, :, :, :], in_=gain_pairs)
+            nc.vector.tensor_copy(
+                out=signed_gains[:, :, :, 0, :],
+                in_=gain_pairs[:, :, :, 0].unsqueeze(3).to_broadcast([P, 2, PAIRS, 2]),
+            )
+            nc.vector.tensor_scalar_mul(out=signed_gains[:, :, :, 1, 0], in0=gain_pairs[:, :, :, 1], scalar1=-1.0)
+            nc.vector.tensor_copy(out=signed_gains[:, :, :, 1, 1], in_=gain_pairs[:, :, :, 1])
 
-        def build_table(engine, qk, e, part):
-            turn_t, turn_h, turn_w = ((cs_t, cs_h, cs_w), (sc_t, sc_h, sc_w))[e]
-            gain = signed_gains[:, e, qk, :, :].rearrange("p pr two -> p (pr two)")
-            if part == 0:
-                engine.tensor_tensor(
-                    out=table_t[:, :, qk, e, :],
-                    in0=turn_t[:].rearrange("p (t a) b -> p t (a b)", t=FRAMES),
-                    in1=gain[:, 0:FEAT_T].unsqueeze(1).to_broadcast([P, FRAMES, FEAT_T]),
-                    op=ALU.mult,
-                )
-            elif part == 1:
-                engine.tensor_tensor(
-                    out=table_hw[:, :, qk, e, 0:FEAT_H],
-                    in0=turn_h[:].rearrange("p a b -> p (a b)").unsqueeze(1).to_broadcast([P, SLOTS, FEAT_H]),
-                    in1=gain[:, FEAT_T : FEAT_T + FEAT_H].unsqueeze(1).to_broadcast([P, SLOTS, FEAT_H]),
-                    op=ALU.mult,
-                )
-            else:
-                engine.tensor_tensor(
-                    out=table_hw[:, :, qk, e, FEAT_H : FEAT_H + FEAT_W],
-                    in0=turn_w[:].rearrange("p (j a) b -> p j (a b)", j=SLOTS),
-                    in1=gain[:, FEAT_T + FEAT_H : HD].unsqueeze(1).to_broadcast([P, SLOTS, FEAT_W]),
-                    op=ALU.mult,
-                )
+        def build_table(engine, qk, part):
+            row0, count, turns, pair0, pairs = (
+                (0, FRAMES, turns_t[:].rearrange("p (r a) two e -> p r (a two e)", r=FRAMES), 0, PAIRS_T),
+                (0, FRAMES, turns_h[:, 0:PAIRS_H0].rearrange("p a two e -> p (a two e)"), PAIRS_T, PAIRS_H0),
+                (FRAMES, SLOTS, turns_h[:, PAIRS_H0:].rearrange("p a two e -> p (a two e)"), PAIRS // 2, PAIRS_H - PAIRS_H0),
+                (FRAMES, SLOTS, turns_w[:].rearrange("p (r a) two e -> p r (a two e)", r=SLOTS), PAIRS - PAIRS_W, PAIRS_W),
+            )[part]
+            if part in (1, 2):
+                turns = turns.unsqueeze(1).to_broadcast([P, count, 4 * pairs])
+            first = 2 * (pair0 % (PAIRS // 2))
+            engine.tensor_tensor(
+                out=tables[:, row0 : row0 + count, qk, first : first + 2 * pairs, :].rearrange("p r f e -> p r (f e)"),
+                in0=turns,
+                in1=signed_gains[:, qk, pair0 : pair0 + pairs, :, :]
+                .rearrange("p a two e -> p (a two e)")
+                .unsqueeze(1)
+                .to_broadcast([P, count, 4 * pairs]),
+                op=ALU.mult,
+            )
 
         prepare_tables()
-        for e in range(2):
-            for part in (1, 2):
-                build_table(nc.gpsimd, 1, e, part)
-        vector_pieces = [(0, e, part) for part in (1, 2, 0) for e in range(2)] + [(1, e, 0) for e in range(2)]
+        for part in (2, 3, 1):
+            build_table(nc.gpsimd, 1, part)
+        vector_pieces = [[(0, 2), (0, 3)], [(0, 1), (0, 0)], [(1, 0)]]
 
         def tables_behind_quantise(step):
-            for qk, e, part in vector_pieces[3 * step - (step > 0) : 3 * step + 2]:
-                build_table(nc.vector, qk, e, part)
+            for qk, part in vector_pieces[step]:
+                build_table(nc.vector, qk, part)
 
         x_t_banks, grouped_tiles, x_mx, acc_banks, v_t_tiles = {}, {}, {}, {}, {}
         v_banks, sumsq_tiles, rstd_tiles, product_tiles, rotated_tiles = {}, {}, {}, {}, {}
@@ -274,25 +269,17 @@ def tile_multiheadattention_pa_t_kernel(
 
         def rotate_products(g, half):
             t, j0 = groups[g]
-            products = stream.tile([P, 2, HALF, 2, HD], F32, bufs=3 * HALVES)
+            products = stream.tile([P, 2, HALF, HD, 2], F32, bufs=3 * HALVES)
             product_tiles[g, half] = products
             for s in range(HALF):
+                row = FRAMES + j0 + half * HALF + s
                 for qk in range(2):
                     v = v_banks[g][half][:, s, qk, :]
-                    scale = rstd_tiles[g, half][:, half, s, qk : qk + 1]
                     nc.vector.scalar_tensor_tensor(
-                        out=products[:, qk, s, :, 0:FEAT_T],
-                        in0=v[:, 0:FEAT_T].unsqueeze(1).to_broadcast([P, 2, FEAT_T]),
-                        scalar=scale,
-                        in1=table_t[:, t, qk, :, :],
-                        op0=ALU.mult,
-                        op1=ALU.mult,
-                    )
-                    nc.vector.scalar_tensor_tensor(
-                        out=products[:, qk, s, :, FEAT_T:HD],
-                        in0=v[:, FEAT_T:HD].unsqueeze(1).to_broadcast([P, 2, HD - FEAT_T]),
-                        scalar=scale,
-                        in1=table_hw[:, j0 + half * HALF + s, qk, :, :],
+                        out=products[:, qk, s, :, :].rearrange("p (b f) e -> p b f e", b=2),
+                        in0=v.rearrange("p (b f) -> p b f", b=2).unsqueeze(3).to_broadcast([P, 2, HALF_HD, 2]),
+                        scalar=rstd_tiles[g, half][:, half, s, qk : qk + 1],
+                        in1=tables[:, t : row + 1 : row - t, qk, :, :],
                         op0=ALU.mult,
                         op1=ALU.mult,
                     )
@@ -302,7 +289,7 @@ def tile_multiheadattention_pa_t_kernel(
             rotated_tiles[g] = rotated
             sums = rotated[:].rearrange("p q s (pr e) -> p q s pr e", e=2)
             for half in range(HALVES):
-                terms = product_tiles[g, half][:].rearrange("p q s e (pr two) -> p two q s pr e", two=2)
+                terms = product_tiles[g, half][:].rearrange("p q s (pr two) e -> p two q s pr e", two=2)
                 slots = slice(half * HALF, (half + 1) * HALF)
                 if g != last:
                     nc.gpsimd.tensor_tensor(out=sums[:, :, slots], in0=terms[:, 0], in1=terms[:, 1], op=ALU.add)

@@ -29,6 +29,15 @@ HALF_HD = HD // 2
 PAIRS_H0 = PAIRS // 2 - PAIRS_T
 EPS = 1e-6
 
+T_COLS = slice(0, FRAMES * 2 * PAIRS_T)
+GAIN_COLS = slice(352, 352 + 2 * HD)
+H_COLS = slice(608, 608 + 2 * PAIRS_H)
+W_COLS = slice(656, 656 + SLOTS * 2 * PAIRS_W)
+BIAS_COLS = slice(992, 992 + HD)
+ROW_WIDTH = 992 + HD
+BIAS_START = 384
+H_START = 384
+
 FLOPS = 2 * 8192 * D * 2 * HD
 
 
@@ -61,6 +70,19 @@ def tile_multiheadattention_pa_t_kernel(
 
         load(0)
 
+        rows = consts.tile([P, ROW_WIDTH], BF16)
+        nc.vector.memset(rows[:].bitcast(I32), 0)
+        for row0, columns, source in (
+            (0, T_COLS, freqs_t.rearrange("t a b -> (t a b)").unsqueeze(0)),
+            (0, W_COLS, freqs_w.rearrange("(wh j) a b -> wh (j a b)", j=SLOTS)),
+            (0, H_COLS, freqs_h.rearrange("h a b -> h (a b)")),
+            (0, slice(GAIN_COLS.start, GAIN_COLS.start + HD), q_scale.unsqueeze(0)),
+            (0, slice(GAIN_COLS.start + HD, GAIN_COLS.stop), k_scale.unsqueeze(0)),
+            (0, BIAS_COLS, bq.unsqueeze(0)),
+            (1, BIAS_COLS, bk.unsqueeze(0)),
+        ):
+            nc.scalar.dma_start(out=rows[row0 : row0 + source.shape[0], columns], in_=source)
+
         w_codes = consts.tile([P, 2, HD], U32, align_bytes=64)
         w_planes = consts.tile([P, 2, HD], U8, align_bytes=64)
         nc.vector.memset(w_planes[:].rearrange("p a n -> p (a n)").bitcast(I32), 0)
@@ -83,39 +105,59 @@ def tile_multiheadattention_pa_t_kernel(
 
         eps_col = consts.tile([P, 1], F32)
         nc.vector.memset(eps_col[:], EPS)
-        gains = consts.tile([P, 2, HD], BF16)
-        nc.scalar.dma_start(out=gains[:, 0, :], in_=q_scale.partition_broadcast(P))
-        nc.scalar.dma_start(out=gains[:, 1, :], in_=k_scale.partition_broadcast(P))
-        cs_t = consts.tile([P, FRAMES * PAIRS_T, 2], BF16)
-        nc.scalar.dma_start(
-            out=cs_t[:].rearrange("p a b -> p (a b)"),
-            in_=freqs_t.rearrange("t a b -> (t a b)").partition_broadcast(P),
+        ident_bf16 = consts.tile([P, P], BF16)
+        nc.vector.tensor_copy(out=ident_bf16[:], in_=ident[:])
+        select_h = consts.tile([P, P], BF16)
+        nc.vector.tensor_copy(
+            out=select_h[:].rearrange("p (h r) -> p h r", r=4),
+            in_=ident_bf16[:, 0:32].unsqueeze(2).to_broadcast([P, 32, 4]),
         )
-        cs_h = consts.tile([P, PAIRS_H, 2], BF16)
-        nc.scalar.dma_start(
-            out=cs_h[:].rearrange("p a b -> p (a b)"),
-            in_=freqs_h.rearrange("h a b -> h (a b)").unsqueeze(1).to_broadcast([32, 4, 2 * PAIRS_H]),
+        select_w = consts.tile([P, P], BF16)
+        nc.vector.tensor_copy(
+            out=select_w[:].rearrange("p (h r) -> p h r", r=4),
+            in_=ident_bf16[:, 0:4].unsqueeze(1).to_broadcast([P, 32, 4]),
         )
-        cs_w = consts.tile([P, SLOTS * PAIRS_W, 2], BF16)
-        nc.scalar.dma_start(
-            out=cs_w[:].rearrange("p a b -> p (a b)"),
-            in_=freqs_w.rearrange("(wh j) a b -> wh (j a b)", j=SLOTS)
-            .unsqueeze(0)
-            .to_broadcast([32, 4, SLOTS * 2 * PAIRS_W]),
-        )
-
-        bias_rows = consts.tile([P, HD], BF16)
-        nc.vector.memset(bias_rows[:], 0.0)
-        nc.scalar.dma_start(out=bias_rows[0:1, :], in_=bq.unsqueeze(0))
-        nc.scalar.dma_start(out=bias_rows[1:2, :], in_=bk.unsqueeze(0))
-        bias_rows_f32 = consts.tile([P, HD], F32)
-        nc.vector.tensor_copy(out=bias_rows_f32[:], in_=bias_rows[:])
         bias_col = consts.tile([P, 2], F32)
 
-        def transpose_bias():
-            bias_ps = psum.tile([P, HALF, 2, HD], F32, tag="v", bufs=4)
-            nc.tensor.transpose(bias_ps[:, 0, 0, :], bias_rows_f32[:], ident[:])
-            nc.vector.tensor_copy(out=bias_col[:], in_=bias_ps[:, 0, 0, 0:2])
+        minus_row = consts.tile([P, 1], BF16)
+        nc.vector.tensor_scalar_mul(out=minus_row[:], in0=ident_bf16[:, 0:1], scalar1=-1.0)
+        spread_banks = {}
+
+        def pairs_of(columns):
+            return rows[:, columns].rearrange("p (a b) -> p a b", b=2)
+
+        def spread(out, selection, values):
+            nc.tensor.matmul(out, lhsT=selection, rhs=values, start=True, stop=True)
+
+        def spread_turns(name, offset, columns, selection, new=True):
+            count = columns.stop - columns.start
+            if new:
+                bank = psum.tile([P, HALF * 2 * HD], F32, tag="v", bufs=4)
+                spread_banks[name] = bank
+            out = spread_banks[name][:, offset : offset + 2 * count].rearrange("p (a two e) -> p a two e", two=2, e=2)
+            given = pairs_of(columns)
+            spread(out[:, :, 0, :], selection, given)
+            for e in range(2):
+                spread(out[:, :, 1, e], selection, given[:, :, 1 - e])
+
+        def spread_rows():
+            first_row = ident_bf16[:, 0:1].to_broadcast([P, P])
+            gains_bank = psum.tile([P, GROUP * P], F32, tag="acc", bufs=2)
+            spread_banks["gains"] = gains_bank
+            out = gains_bank[:].rearrange("p (a two e) -> p a two e", two=2, e=2)
+            given = pairs_of(GAIN_COLS)
+            for e in range(2):
+                spread(out[:, :, 0, e], first_row, given[:, :, 0])
+            spread(out[:, :, 1, 0], minus_row[:].to_broadcast([P, P]), given[:, :, 1])
+            spread(out[:, :, 1, 1], first_row, given[:, :, 1])
+            w_half = slice(W_COLS.start, W_COLS.start + SLOTS * PAIRS_W), slice(W_COLS.start + SLOTS * PAIRS_W, W_COLS.stop)
+            spread_turns("w0", 0, w_half[0], select_w[:])
+            spread(spread_banks["w0"][:, BIAS_START : BIAS_START + 2], rows[:, BIAS_COLS], ident_bf16[:, 0:2])
+            spread_turns("w1", 0, w_half[1], select_w[:])
+            spread_turns("w1", H_START, H_COLS, select_h[:], new=False)
+            for half in range(2):
+                first = T_COLS.start + half * FRAMES * PAIRS_T
+                spread_turns("t%d" % half, 0, slice(first, first + FRAMES * PAIRS_T), first_row)
 
         table_warm_up = consts.tile([P, 1], F32)
         nc.scalar.activation(out=table_warm_up[:], in_=eps_col[:], func=ACT.Abs_reciprocal_sqrt)
@@ -126,18 +168,27 @@ def tile_multiheadattention_pa_t_kernel(
         signed_gains = consts.tile([P, 2, PAIRS, 2, 2], F32)
         tables = consts.tile([P, FRAMES + SLOTS, 2, HALF_HD, 2], F32)
 
-        def prepare_tables():
-            for turns, given in ((turns_t, cs_t), (turns_h, cs_h), (turns_w, cs_w)):
-                nc.vector.tensor_copy(out=turns[:, :, 0, :], in_=given[:])
-                for e in range(2):
-                    nc.vector.tensor_copy(out=turns[:, :, 1, e], in_=given[:, :, 1 - e])
-            gain_pairs = gains[:].rearrange("p q (pr two) -> p q pr two", two=2)
-            nc.vector.tensor_copy(
-                out=signed_gains[:, :, :, 0, :],
-                in_=gain_pairs[:, :, :, 0].unsqueeze(3).to_broadcast([P, 2, PAIRS, 2]),
+        def prepare_gains_hw():
+            nc.scalar.copy(out=signed_gains[:].rearrange("p q pr two e -> p (q pr two e)"), in_=spread_banks["gains"][:])
+            half = SLOTS * PAIRS_W // 2
+            nc.scalar.copy(
+                out=turns_h[:].rearrange("p a two e -> p (a two e)"),
+                in_=spread_banks["w1"][:, H_START : H_START + 4 * PAIRS_H],
             )
-            nc.vector.tensor_scalar_mul(out=signed_gains[:, :, :, 1, 0], in0=gain_pairs[:, :, :, 1], scalar1=-1.0)
-            nc.vector.tensor_copy(out=signed_gains[:, :, :, 1, 1], in_=gain_pairs[:, :, :, 1])
+            for i in range(2):
+                nc.scalar.copy(
+                    out=turns_w[:, i * half : (i + 1) * half].rearrange("p a two e -> p (a two e)"),
+                    in_=spread_banks["w%d" % i][:, 0 : 4 * half],
+                )
+
+        def prepare_bias_t():
+            nc.vector.tensor_copy(out=bias_col[:], in_=spread_banks["w0"][:, BIAS_START : BIAS_START + 2])
+            half = FRAMES * PAIRS_T // 2
+            for i in range(2):
+                nc.vector.tensor_copy(
+                    out=turns_t[:, i * half : (i + 1) * half].rearrange("p a two e -> p (a two e)"),
+                    in_=spread_banks["t%d" % i][:, 0 : 4 * half],
+                )
 
         def build_table(engine, qk, part):
             row0, count, turns, pair0, pairs = (
@@ -159,9 +210,10 @@ def tile_multiheadattention_pa_t_kernel(
                 op=ALU.mult,
             )
 
-        prepare_tables()
-        for part in (2, 3, 1):
-            build_table(nc.gpsimd, 1, part)
+        def tables_ahead():
+            for part in (2, 3, 1):
+                build_table(nc.gpsimd, 1, part)
+
         vector_pieces = [[(0, 2), (0, 3)], [(0, 1), (0, 0)], [(1, 0)]]
 
         def tables_behind_quantise(step):
@@ -310,14 +362,19 @@ def tile_multiheadattention_pa_t_kernel(
 
         with tc.manual_schedule():
             transpose_x(0)
-            transpose_bias()
+            spread_rows()
             for step in range(n_groups + 4):
                 when(step + LOADS_AHEAD, load)
                 when(step, copy_x)
+                if step == 0:
+                    prepare_gains_hw()
+                    tables_ahead()
                 when(step - 3, inverse_rms)
                 when(step + 1, transpose_x)
                 when(step - 3, rotate_products, 0)
                 when(step, quantise_x)
+                if step == 0:
+                    prepare_bias_t()
                 if step < 3:
                     tables_behind_quantise(step)
                 when(step - 1, add_bias)

@@ -240,7 +240,7 @@ def tile_multiheadattention_pa_t_kernel(
             grouped_tiles[g] = grouped
             words = grouped[:].bitcast(F32).rearrange("p (h n u) -> p h n u", h=HALVES, u=2)
             for half in range(HALVES):
-                copy = nc.vector.tensor_copy if (g % 2 == 1 and half == 1) else nc.scalar.copy
+                copy = nc.vector.tensor_copy if (half == 1 and g < n_groups - 2) else nc.scalar.copy
                 copy(out=words[:, half, :, :], in_=x_t_banks[g][half][:].rearrange("p u n -> p n u"))
 
         def quantise_x(g):

@@ -117,108 +117,108 @@ def tile_multiheadattention_pa_t_kernel(
             out=select_w[:].rearrange("p (h r) -> p h r", r=4),
             in_=ident_bf16[:, 0:4].unsqueeze(1).to_broadcast([P, 32, 4]),
         )
+        feature_order = consts.tile([P, P], F32)
+        nc.vector.tensor_copy(
+            out=feature_order[:].rearrange("p (b two pr) -> p b two pr", b=2, two=2),
+            in_=ident[:].rearrange("p (b pr two) -> p b two pr", b=2, two=2),
+        )
         bias_col = consts.tile([P, 2], F32)
 
         minus_row = consts.tile([P, 1], BF16)
         nc.vector.tensor_scalar_mul(out=minus_row[:], in0=ident_bf16[:, 0:1], scalar1=-1.0)
         spread_banks = {}
 
-        def pairs_of(columns):
-            return rows[:, columns].rearrange("p (a b) -> p a b", b=2)
-
         def spread(out, selection, values):
             nc.tensor.matmul(out, lhsT=selection, rhs=values, start=True, stop=True)
 
-        def spread_turns(name, offset, columns, selection, new=True):
-            count = columns.stop - columns.start
-            if new:
-                bank = psum.tile([P, HALF * 2 * HD], F32, tag="v", bufs=4)
-                spread_banks[name] = bank
-            out = spread_banks[name][:, offset : offset + 2 * count].rearrange("p (a two e) -> p a two e", two=2, e=2)
-            given = pairs_of(columns)
-            spread(out[:, :, 0, :], selection, given)
+        def spread_turns(bank, offset, columns, count, selection):
+            given = rows[:, columns].rearrange("p (r a e) -> p r a e", r=count, e=2)
+            width = 2 * (columns.stop - columns.start)
+            out = bank[:, offset : offset + width].rearrange("p (r two a e) -> p r two a e", r=count, two=2, e=2)
+            spread(out[:, :, 0].rearrange("p r a e -> p r (a e)"), selection, given.rearrange("p r a e -> p r (a e)"))
             for e in range(2):
-                spread(out[:, :, 1, e], selection, given[:, :, 1 - e])
+                spread(out[:, :, 1, :, e], selection, given[:, :, :, 1 - e])
+
+        def spread_halves(name, columns, count, selection):
+            for half in range(2):
+                bank = psum.tile([P, HALF * 2 * HD], F32, tag="v", bufs=4)
+                spread_banks[name, half] = bank
+                width = (columns.stop - columns.start) // 2
+                start = columns.start + half * width
+                spread_turns(bank, 0, slice(start, start + width), count // 2, selection)
 
         def spread_rows():
             first_row = ident_bf16[:, 0:1].to_broadcast([P, P])
             gains_bank = psum.tile([P, GROUP * P], F32, tag="acc", bufs=2)
             spread_banks["gains"] = gains_bank
-            out = gains_bank[:].rearrange("p (a two e) -> p a two e", two=2, e=2)
-            given = pairs_of(GAIN_COLS)
+            out = gains_bank[:].rearrange("p (q two pr e) -> p q two pr e", q=4, two=2, e=2)
+            given = rows[:, GAIN_COLS].rearrange("p (q pr two) -> p q pr two", q=4, two=2)
             for e in range(2):
-                spread(out[:, :, 0, e], first_row, given[:, :, 0])
-            spread(out[:, :, 1, 0], minus_row[:].to_broadcast([P, P]), given[:, :, 1])
-            spread(out[:, :, 1, 1], first_row, given[:, :, 1])
-            w_half = slice(W_COLS.start, W_COLS.start + SLOTS * PAIRS_W), slice(W_COLS.start + SLOTS * PAIRS_W, W_COLS.stop)
-            spread_turns("w0", 0, w_half[0], select_w[:])
-            spread(spread_banks["w0"][:, BIAS_START : BIAS_START + 2], rows[:, BIAS_COLS], ident_bf16[:, 0:2])
-            spread_turns("w1", 0, w_half[1], select_w[:])
-            spread_turns("w1", H_START, H_COLS, select_h[:], new=False)
-            for half in range(2):
-                first = T_COLS.start + half * FRAMES * PAIRS_T
-                spread_turns("t%d" % half, 0, slice(first, first + FRAMES * PAIRS_T), first_row)
+                spread(out[:, :, 0, :, e], first_row, given[:, :, :, 0])
+            spread(out[:, :, 1, :, 0], minus_row[:].to_broadcast([P, P]), given[:, :, :, 1])
+            spread(out[:, :, 1, :, 1], first_row, given[:, :, :, 1])
+            spread_halves("w", W_COLS, SLOTS, select_w[:])
+            h_split = H_COLS.start + 2 * PAIRS_H0
+            spread_turns(spread_banks["w", 1], H_START, slice(H_COLS.start, h_split), 1, select_h[:])
+            spread_turns(spread_banks["w", 1], H_START + 4 * PAIRS_H0, slice(h_split, H_COLS.stop), 1, select_h[:])
+            spread(spread_banks["w", 0][:, BIAS_START : BIAS_START + 2], rows[:, BIAS_COLS], ident_bf16[:, 0:2])
+            spread_halves("t", T_COLS, FRAMES, first_row)
 
         table_warm_up = consts.tile([P, 1], F32)
         nc.scalar.activation(out=table_warm_up[:], in_=eps_col[:], func=ACT.Abs_reciprocal_sqrt)
 
-        turns_t = consts.tile([P, FRAMES * PAIRS_T, 2, 2], BF16)
-        turns_h = consts.tile([P, PAIRS_H, 2, 2], BF16)
-        turns_w = consts.tile([P, SLOTS * PAIRS_W, 2, 2], BF16)
-        signed_gains = consts.tile([P, 2, PAIRS, 2, 2], F32)
-        tables = consts.tile([P, FRAMES + SLOTS, 2, HALF_HD, 2], F32)
+        turns_t = consts.tile([P, FRAMES, 2, 2 * PAIRS_T], BF16)
+        turns_h = consts.tile([P, 4 * PAIRS_H], BF16)
+        turns_w = consts.tile([P, SLOTS, 2, 2 * PAIRS_W], BF16)
+        signed_gains = consts.tile([P, 2, 2, 2, HALF_HD], F32)
+        tables = consts.tile([P, FRAMES + SLOTS, 2, 2, HALF_HD], F32)
 
         def prepare_gains_hw():
-            nc.scalar.copy(out=signed_gains[:].rearrange("p q pr two e -> p (q pr two e)"), in_=spread_banks["gains"][:])
-            half = SLOTS * PAIRS_W // 2
-            nc.scalar.copy(
-                out=turns_h[:].rearrange("p a two e -> p (a two e)"),
-                in_=spread_banks["w1"][:, H_START : H_START + 4 * PAIRS_H],
-            )
+            nc.scalar.copy(out=signed_gains[:].rearrange("p q b two n -> p (q b two n)"), in_=spread_banks["gains"][:])
+            half = SLOTS // 2
             for i in range(2):
                 nc.scalar.copy(
-                    out=turns_w[:, i * half : (i + 1) * half].rearrange("p a two e -> p (a two e)"),
-                    in_=spread_banks["w%d" % i][:, 0 : 4 * half],
+                    out=turns_w[:, i * half : (i + 1) * half].rearrange("p r two n -> p (r two n)"),
+                    in_=spread_banks["w", i][:, 0 : half * 4 * PAIRS_W],
                 )
+            nc.scalar.copy(out=turns_h[:], in_=spread_banks["w", 1][:, H_START : H_START + 4 * PAIRS_H])
 
         def prepare_bias_t():
-            nc.vector.tensor_copy(out=bias_col[:], in_=spread_banks["w0"][:, BIAS_START : BIAS_START + 2])
-            half = FRAMES * PAIRS_T // 2
+            nc.vector.tensor_copy(out=bias_col[:], in_=spread_banks["w", 0][:, BIAS_START : BIAS_START + 2])
+            half = FRAMES // 2
             for i in range(2):
                 nc.vector.tensor_copy(
-                    out=turns_t[:, i * half : (i + 1) * half].rearrange("p a two e -> p (a two e)"),
-                    in_=spread_banks["t%d" % i][:, 0 : 4 * half],
+                    out=turns_t[:, i * half : (i + 1) * half].rearrange("p r two n -> p (r two n)"),
+                    in_=spread_banks["t", i][:, 0 : half * 4 * PAIRS_T],
                 )
 
         def build_table(engine, qk, part):
-            row0, count, turns, pair0, pairs = (
-                (0, FRAMES, turns_t[:].rearrange("p (r a) two e -> p r (a two e)", r=FRAMES), 0, PAIRS_T),
-                (0, FRAMES, turns_h[:, 0:PAIRS_H0].rearrange("p a two e -> p (a two e)"), PAIRS_T, PAIRS_H0),
-                (FRAMES, SLOTS, turns_h[:, PAIRS_H0:].rearrange("p a two e -> p (a two e)"), PAIRS // 2, PAIRS_H - PAIRS_H0),
-                (FRAMES, SLOTS, turns_w[:].rearrange("p (r a) two e -> p r (a two e)", r=SLOTS), PAIRS - PAIRS_W, PAIRS_W),
+            row0, count, turns, first, pairs = (
+                (0, FRAMES, turns_t[:], 0, PAIRS_T),
+                (0, FRAMES, turns_h[:, 0 : 4 * PAIRS_H0], PAIRS_T, PAIRS_H0),
+                (FRAMES, SLOTS, turns_h[:, 4 * PAIRS_H0 :], 0, PAIRS_H - PAIRS_H0),
+                (FRAMES, SLOTS, turns_w[:], PAIRS_H - PAIRS_H0, PAIRS_W),
             )[part]
+            shape = [P, count, 2, 2 * pairs]
+            columns = slice(2 * first, 2 * (first + pairs))
             if part in (1, 2):
-                turns = turns.unsqueeze(1).to_broadcast([P, count, 4 * pairs])
-            first = 2 * (pair0 % (PAIRS // 2))
+                turns = turns.rearrange("p (two n) -> p two n", two=2).unsqueeze(1).to_broadcast(shape)
             engine.tensor_tensor(
-                out=tables[:, row0 : row0 + count, qk, first : first + 2 * pairs, :].rearrange("p r f e -> p r (f e)"),
+                out=tables[:, row0 : row0 + count, qk, :, columns],
                 in0=turns,
-                in1=signed_gains[:, qk, pair0 : pair0 + pairs, :, :]
-                .rearrange("p a two e -> p (a two e)")
-                .unsqueeze(1)
-                .to_broadcast([P, count, 4 * pairs]),
+                in1=signed_gains[:, qk, part // 2, :, columns].unsqueeze(1).to_broadcast(shape),
                 op=ALU.mult,
             )
 
-        def tables_ahead():
-            for part in (2, 3, 1):
+        def tables_of_k():
+            for part in (3, 2, 1, 0):
                 build_table(nc.gpsimd, 1, part)
 
-        vector_pieces = [[(0, 2), (0, 3)], [(0, 1), (0, 0)], [(1, 0)]]
+        vector_pieces = [[2, 3], [1, 0]]
 
-        def tables_behind_quantise(step):
-            for qk, part in vector_pieces[step]:
-                build_table(nc.vector, qk, part)
+        def tables_of_q(step):
+            for part in vector_pieces[step]:
+                build_table(nc.vector, 0, part)
 
         x_t_banks, grouped_tiles, x_mx, acc_banks, v_t_tiles = {}, {}, {}, {}, {}
         v_banks, sumsq_tiles, rstd_tiles, product_tiles, rotated_tiles = {}, {}, {}, {}, {}
@@ -286,7 +286,7 @@ def tile_multiheadattention_pa_t_kernel(
                 for s in range(HALF):
                     for qk in range(2):
                         col = (half * HALF + s) * P
-                        nc.tensor.transpose(v[:, s, qk, :], v_t_tiles[g][:, qk, col : col + P], ident[:])
+                        nc.tensor.transpose(v[:, s, qk, :], v_t_tiles[g][:, qk, col : col + P], feature_order[:])
 
         last = n_groups - 1
 
@@ -321,17 +321,17 @@ def tile_multiheadattention_pa_t_kernel(
 
         def rotate_products(g, half):
             t, j0 = groups[g]
-            products = stream.tile([P, 2, HALF, HD, 2], F32, bufs=3 * HALVES)
+            products = stream.tile([P, 2, HALF, 2, 2, HALF_HD], F32, bufs=3 * HALVES)
             product_tiles[g, half] = products
             for s in range(HALF):
                 row = FRAMES + j0 + half * HALF + s
                 for qk in range(2):
                     v = v_banks[g][half][:, s, qk, :]
                     nc.vector.scalar_tensor_tensor(
-                        out=products[:, qk, s, :, :].rearrange("p (b f) e -> p b f e", b=2),
+                        out=products[:, qk, s].rearrange("p b two (pr e) -> p b (two pr) e", e=2),
                         in0=v.rearrange("p (b f) -> p b f", b=2).unsqueeze(3).to_broadcast([P, 2, HALF_HD, 2]),
                         scalar=rstd_tiles[g, half][:, half, s, qk : qk + 1],
-                        in1=tables[:, t : row + 1 : row - t, qk, :, :],
+                        in1=tables[:, t : row + 1 : row - t, qk].rearrange("p b two (pr e) -> p b (two pr) e", e=2),
                         op0=ALU.mult,
                         op1=ALU.mult,
                     )
@@ -339,9 +339,9 @@ def tile_multiheadattention_pa_t_kernel(
         def rotate_add(g):
             rotated = stream.tile([P, 2, GROUP, HD], F32)
             rotated_tiles[g] = rotated
-            sums = rotated[:].rearrange("p q s (pr e) -> p q s pr e", e=2)
+            sums = rotated[:].rearrange("p q s (b n) -> p q s b n", b=2)
             for half in range(HALVES):
-                terms = product_tiles[g, half][:].rearrange("p q s (pr two) e -> p two q s pr e", two=2)
+                terms = product_tiles[g, half][:].rearrange("p q s b two n -> p two q s b n")
                 slots = slice(half * HALF, (half + 1) * HALF)
                 if g != last:
                     nc.gpsimd.tensor_tensor(out=sums[:, :, slots], in0=terms[:, 0], in1=terms[:, 1], op=ALU.add)
@@ -368,15 +368,15 @@ def tile_multiheadattention_pa_t_kernel(
                 when(step, copy_x)
                 if step == 0:
                     prepare_gains_hw()
-                    tables_ahead()
                 when(step - 3, inverse_rms)
                 when(step + 1, transpose_x)
                 when(step - 3, rotate_products, 0)
                 when(step, quantise_x)
                 if step == 0:
                     prepare_bias_t()
-                if step < 3:
-                    tables_behind_quantise(step)
+                    tables_of_k()
+                if step < len(vector_pieces):
+                    tables_of_q(step)
                 when(step - 1, add_bias)
                 when(step, project)
                 when(step - 2, norm)

@@ -21,7 +21,7 @@ SLOTS = 8
 GROUP = 4
 HALF = 2
 HALVES = GROUP // HALF
-LOADS_AHEAD = 3
+LOADS_AHEAD = 6
 PAIRS_T = 22
 PAIRS_H = 21
 PAIRS_W = 21
@@ -60,33 +60,23 @@ def tile_multiheadattention_pa_t_kernel(
         n_groups = len(groups)
         x_tiles = {}
 
-        def load(g):
+        def load(g, pieces=1):
             t, j0 = groups[g]
-            x_sb = stream.tile([P, GROUP, D], BF16, bufs=5)
-            for half in range(HALVES):
-                slots = slice(half * HALF, (half + 1) * HALF)
+            x_sb = stream.tile([P, GROUP, D], BF16, bufs=6)
+            for i in range(pieces):
+                slots = slice(i * GROUP // pieces, (i + 1) * GROUP // pieces)
                 nc.sync.dma_start(out=x_sb[:, slots, :], in_=x_frames[t, :, j0:, :][:, slots, :])
             x_tiles[g] = x_sb
 
         load(0)
 
-        rows = consts.tile([P, ROW_WIDTH], BF16)
-        nc.vector.memset(rows[:].bitcast(I32), 0)
-        for row0, columns, source in (
-            (0, T_COLS, freqs_t.rearrange("t a b -> (t a b)").unsqueeze(0)),
-            (0, W_COLS, freqs_w.rearrange("(wh j) a b -> wh (j a b)", j=SLOTS)),
-            (0, H_COLS, freqs_h.rearrange("h a b -> h (a b)")),
-            (0, slice(GAIN_COLS.start, GAIN_COLS.start + HD), q_scale.unsqueeze(0)),
-            (0, slice(GAIN_COLS.start + HD, GAIN_COLS.stop), k_scale.unsqueeze(0)),
-            (0, BIAS_COLS, bq.unsqueeze(0)),
-            (1, BIAS_COLS, bk.unsqueeze(0)),
-        ):
-            nc.scalar.dma_start(out=rows[row0 : row0 + source.shape[0], columns], in_=source)
-
         w_codes = consts.tile([P, 2, HD], U32, align_bytes=64)
         w_planes = consts.tile([P, 2, HD], U8, align_bytes=64)
         nc.vector.memset(w_planes[:].rearrange("p a n -> p (a n)").bitcast(I32), 0)
-        for qk, (words, scales) in enumerate(((Wq_words, Wq_scales), (Wk_words, Wk_scales))):
+        rows = consts.tile([P, ROW_WIDTH], BF16)
+        nc.vector.memset(rows[:].bitcast(I32), 0)
+
+        def load_weight(qk, words, scales):
             nc.sync.dma_start(
                 out=w_codes[:, qk, :].bitcast(I32),
                 in_=words.rearrange("g p n t -> (g p) (n t)").bitcast(I32),
@@ -97,9 +87,23 @@ def tile_multiheadattention_pa_t_kernel(
                     in_=scales[0, 4 * quad : 4 * quad + 4, :].bitcast(I32),
                 )
 
-        for g in range(1, LOADS_AHEAD):
-            load(g)
+        def load_rows(row0, columns, source):
+            nc.sync.dma_start(out=rows[row0 : row0 + source.shape[0], columns], in_=source)
 
+        load_rows(0, W_COLS, freqs_w.rearrange("(wh j) a b -> wh (j a b)", j=SLOTS))
+        load_rows(0, H_COLS, freqs_h.rearrange("h a b -> h (a b)"))
+        load_rows(0, slice(GAIN_COLS.start, GAIN_COLS.start + HD), q_scale.unsqueeze(0))
+        load_rows(0, slice(GAIN_COLS.start + HD, GAIN_COLS.stop), k_scale.unsqueeze(0))
+        load_rows(0, T_COLS, freqs_t.rearrange("t a b -> (t a b)").unsqueeze(0))
+        load(1)
+        load_rows(0, BIAS_COLS, bq.unsqueeze(0))
+        load_rows(1, BIAS_COLS, bk.unsqueeze(0))
+        load_weight(0, Wq_words, Wq_scales)
+        load_weight(1, Wk_words, Wk_scales)
+        load(2)
+        load(3)
+        load(4)
+        load(5)
         ident = consts.tile([P, P], F32)
         make_identity(nc, ident[:])
 
@@ -162,63 +166,57 @@ def tile_multiheadattention_pa_t_kernel(
             spread_turns(spread_banks["w", 1], H_START, slice(H_COLS.start, h_split), 1, select_h[:])
             spread_turns(spread_banks["w", 1], H_START + 4 * PAIRS_H0, slice(h_split, H_COLS.stop), 1, select_h[:])
             spread(spread_banks["w", 0][:, BIAS_START : BIAS_START + 2], rows[:, BIAS_COLS], ident_bf16[:, 0:2])
-            spread_halves("t", T_COLS, FRAMES, first_row)
+
+        def spread_t():
+            spread_halves("t", T_COLS, FRAMES, ident_bf16[:, 0:1].to_broadcast([P, P]))
 
         table_warm_up = consts.tile([P, 1], F32)
         nc.scalar.activation(out=table_warm_up[:], in_=eps_col[:], func=ACT.Abs_reciprocal_sqrt)
 
-        turns_t = consts.tile([P, FRAMES, 2, 2 * PAIRS_T], BF16)
-        turns_h = consts.tile([P, 4 * PAIRS_H], BF16)
-        turns_w = consts.tile([P, SLOTS, 2, 2 * PAIRS_W], BF16)
         signed_gains = consts.tile([P, 2, 2, 2, HALF_HD], F32)
         tables = consts.tile([P, FRAMES + SLOTS, 2, 2, HALF_HD], F32)
 
-        def prepare_gains_hw():
+        turns = {
+            name: consts.tile([P, width], BF16, name="turns_" + name)
+            for name, width in (("w", SLOTS * 4 * PAIRS_W), ("h", 4 * PAIRS_H), ("t", FRAMES * 4 * PAIRS_T))
+        }
+
+        def copy_gains_hw():
             nc.scalar.copy(out=signed_gains[:].rearrange("p q b two n -> p (q b two n)"), in_=spread_banks["gains"][:])
-            half = SLOTS // 2
-            for i in range(2):
-                nc.scalar.copy(
-                    out=turns_w[:, i * half : (i + 1) * half].rearrange("p r two n -> p (r two n)"),
-                    in_=spread_banks["w", i][:, 0 : half * 4 * PAIRS_W],
-                )
-            nc.scalar.copy(out=turns_h[:], in_=spread_banks["w", 1][:, H_START : H_START + 4 * PAIRS_H])
 
-        def prepare_bias_t():
-            nc.vector.tensor_copy(out=bias_col[:], in_=spread_banks["w", 0][:, BIAS_START : BIAS_START + 2])
-            half = FRAMES // 2
-            for i in range(2):
-                nc.vector.tensor_copy(
-                    out=turns_t[:, i * half : (i + 1) * half].rearrange("p r two n -> p (r two n)"),
-                    in_=spread_banks["t", i][:, 0 : half * 4 * PAIRS_T],
-                )
+        def copy_turns(name, width):
+            for half in range(2):
+                columns = slice(half * width // 2, (half + 1) * width // 2)
+                nc.scalar.copy(out=turns[name][:, columns], in_=spread_banks[name, half][:, 0 : width // 2])
 
-        def build_table(engine, qk, part):
-            row0, count, turns, first, pairs = (
-                (0, FRAMES, turns_t[:], 0, PAIRS_T),
-                (0, FRAMES, turns_h[:, 0 : 4 * PAIRS_H0], PAIRS_T, PAIRS_H0),
-                (FRAMES, SLOTS, turns_h[:, 4 * PAIRS_H0 :], 0, PAIRS_H - PAIRS_H0),
-                (FRAMES, SLOTS, turns_w[:], PAIRS_H - PAIRS_H0, PAIRS_W),
+        def copy_t():
+            copy_turns("t", FRAMES * 4 * PAIRS_T)
+
+        def table_piece(engine, qk, part, half, direct):
+            row0, name, start, first, pairs = (
+                (0, "t", 0, 0, PAIRS_T),
+                (0, "h", 0, PAIRS_T, PAIRS_H0),
+                (FRAMES, "h", 4 * PAIRS_H0, 0, PAIRS_H - PAIRS_H0),
+                (FRAMES, "w", 0, PAIRS_H - PAIRS_H0, PAIRS_W),
             )[part]
+            halves = 1 if half is None else 2
+            count = 8 // halves
             shape = [P, count, 2, 2 * pairs]
             columns = slice(2 * first, 2 * (first + pairs))
-            if part in (1, 2):
-                turns = turns.rearrange("p (two n) -> p two n", two=2).unsqueeze(1).to_broadcast(shape)
+            row0 += (half or 0) * count
+            if name == "h":
+                given = turns["h"][:, start : start + 4 * pairs] if not direct else spread_banks["w", 1][:, H_START + start : H_START + start + 4 * pairs]
+                given = given.rearrange("p (two n) -> p two n", two=2).unsqueeze(1).to_broadcast(shape)
+            else:
+                width = count * 4 * pairs
+                given = spread_banks[name, half][:, 0:width] if direct else turns[name][:, (half or 0) * width : (half or 0) * width + width]
+                given = given.rearrange("p (r two n) -> p r two n", r=count, two=2)
             engine.tensor_tensor(
                 out=tables[:, row0 : row0 + count, qk, :, columns],
-                in0=turns,
+                in0=given,
                 in1=signed_gains[:, qk, part // 2, :, columns].unsqueeze(1).to_broadcast(shape),
                 op=ALU.mult,
             )
-
-        def tables_of_k():
-            for part in (3, 2, 1, 0):
-                build_table(nc.gpsimd, 1, part)
-
-        vector_pieces = [[2, 3], [1, 0]]
-
-        def tables_of_q(step):
-            for part in vector_pieces[step]:
-                build_table(nc.vector, 0, part)
 
         x_t_banks, grouped_tiles, x_mx, acc_banks, v_t_tiles = {}, {}, {}, {}, {}
         v_banks, sumsq_tiles, rstd_tiles, product_tiles, rotated_tiles = {}, {}, {}, {}, {}
@@ -240,7 +238,7 @@ def tile_multiheadattention_pa_t_kernel(
             grouped_tiles[g] = grouped
             words = grouped[:].bitcast(F32).rearrange("p (h n u) -> p h n u", h=HALVES, u=2)
             for half in range(HALVES):
-                copy = nc.vector.tensor_copy if (half == 1 and g < n_groups - 2) else nc.scalar.copy
+                copy = nc.vector.tensor_copy if half == 1 and g > 2 else nc.scalar.copy
                 copy(out=words[:, half, :, :], in_=x_t_banks[g][half][:].rearrange("p u n -> p n u"))
 
         def quantise_x(g):
@@ -290,34 +288,25 @@ def tile_multiheadattention_pa_t_kernel(
 
         last = n_groups - 1
 
-        def norm(g):
-            squares = stream.tile([P, HALVES, HALF, 2, HD], BF16, bufs=2)
-            sumsq = stream.tile([P, HALVES, HALF, 2], F32)
-            sumsq_tiles[g] = sumsq
-            for half in range(HALVES):
-                for s in range(HALF):
-                    for qk in range(2):
-                        nc.scalar.activation(
-                            out=squares[:, half, s, qk, :],
-                            in_=v_banks[g][half][:, s, qk, :],
-                            func=ACT.Square,
-                            accum_out=sumsq[:, half, s, qk : qk + 1],
-                        )
-                if g == last:
-                    inverse_rms_of(g, half, sumsq[:, half, :, :])
+        def norm(g, half):
+            squares = stream.tile([P, HALF, 2, HD], BF16, bufs=2)
+            sumsq = stream.tile([P, HALF, 2], F32, bufs=4)
+            sumsq_tiles[g, half] = sumsq
+            for s in range(HALF):
+                for qk in range(2):
+                    nc.scalar.activation(
+                        out=squares[:, s, qk, :],
+                        in_=v_banks[g][half][:, s, qk, :],
+                        func=ACT.Square,
+                        accum_out=sumsq[:, s, qk : qk + 1],
+                    )
 
-        def inverse_rms_of(g, half, sums):
-            rstd = stream.tile([P, HALVES, HALF, 2], F32)
-            out = rstd[:] if half is None else rstd[:, half, :, :]
+        def inverse_rms(g, half):
+            rstd = stream.tile([P, HALF, 2], F32, bufs=4)
+            rstd_tiles[g, half] = rstd
             nc.scalar.activation(
-                out=out, in_=sums, func=ACT.Abs_reciprocal_sqrt, bias=eps_col[:, 0:1], scale=1.0 / HD
+                out=rstd[:], in_=sumsq_tiles[g, half][:], func=ACT.Abs_reciprocal_sqrt, bias=eps_col[:, 0:1], scale=1.0 / HD
             )
-            for h in range(HALVES) if half is None else [half]:
-                rstd_tiles[g, h] = rstd
-
-        def inverse_rms(g):
-            if g != last:
-                inverse_rms_of(g, None, sumsq_tiles[g][:])
 
         def rotate_products(g, half):
             t, j0 = groups[g]
@@ -330,7 +319,7 @@ def tile_multiheadattention_pa_t_kernel(
                     nc.vector.scalar_tensor_tensor(
                         out=products[:, qk, s].rearrange("p b two (pr e) -> p b (two pr) e", e=2),
                         in0=v.rearrange("p (b f) -> p b f", b=2).unsqueeze(3).to_broadcast([P, 2, HALF_HD, 2]),
-                        scalar=rstd_tiles[g, half][:, half, s, qk : qk + 1],
+                        scalar=rstd_tiles[g, half][:, s, qk : qk + 1],
                         in1=tables[:, t : row + 1 : row - t, qk].rearrange("p b two (pr e) -> p b (two pr) e", e=2),
                         op0=ALU.mult,
                         op1=ALU.mult,
@@ -362,25 +351,37 @@ def tile_multiheadattention_pa_t_kernel(
 
         with tc.manual_schedule():
             transpose_x(0)
+            copy_x(0)
+            quantise_x(0)
+            transpose_x(1)
             spread_rows()
-            for step in range(n_groups + 4):
+            nc.vector.tensor_copy(out=bias_col[:], in_=spread_banks["w", 0][:, BIAS_START : BIAS_START + 2])
+            copy_gains_hw()
+            for part in (3, 2, 1):
+                for half in ((0, 1) if part == 3 else (None,)):
+                    for qk in range(2):
+                        table_piece(nc.vector, qk, part, half, True)
+            copy_x(1)
+            quantise_x(1)
+            project(0)
+            spread_t()
+            for half in range(2):
+                for qk in range(2):
+                    table_piece(nc.vector, qk, 0, half, True)
+            transpose_x(2)
+            for step in range(n_groups + 2):
                 when(step + LOADS_AHEAD, load)
-                when(step, copy_x)
-                if step == 0:
-                    prepare_gains_hw()
-                when(step - 3, inverse_rms)
-                when(step + 1, transpose_x)
-                when(step - 3, rotate_products, 0)
-                when(step, quantise_x)
-                if step == 0:
-                    prepare_bias_t()
-                    tables_of_k()
-                if step < len(vector_pieces):
-                    tables_of_q(step)
-                when(step - 1, add_bias)
-                when(step, project)
-                when(step - 2, norm)
-                when(step - 3, rotate_products, 1)
-                when(step - 1, transpose_back)
-                when(step - 3, rotate_add)
-                when(step - 3, store)
+                when(step, add_bias)
+                when(step - 1, inverse_rms, 0)
+                when(step - 1, norm, 1)
+                when(step + 2, copy_x)
+                when(step - 1, inverse_rms, 1)
+                when(step, transpose_back)
+                when(step, norm, 0)
+                when(step - 1, rotate_products, 0)
+                when(step - 1, rotate_products, 1)
+                when(step + 2, quantise_x)
+                when(step + 1, project)
+                when(step + 3, transpose_x)
+                when(step - 1, rotate_add)
+                when(step - 1, store)

@@ -379,8 +379,8 @@ def tile_multiheadattention_pa_t_kernel(
                 when(step, transpose_back)
                 when(step, norm, 0)
                 when(step - 1, rotate_products, 0)
-                when(step - 1, rotate_products, 1)
                 when(step + 2, quantise_x)
+                when(step - 1, rotate_products, 1)
                 when(step + 1, project)
                 when(step + 3, transpose_x)
                 when(step - 1, rotate_add)

@@ -265,6 +265,21 @@ def tile_multiheadattention_pa_t_kernel(
                     stop=True,
                 )
 
+        def keep_clock(g):
+            x_codes, x_planes = x_mx[g]
+            bank = psum.tile([P, HALF, 2, HD], F32, tag="v", bufs=4)
+            v_banks[g] = [bank]
+            for qk in range(2):
+                nc.tensor.matmul_mx(
+                    out=bank[:].rearrange("p s q f -> p (s q f)"),
+                    lhsT=w_codes[:, qk, :].bitcast(FP8X4),
+                    lhsT_scale=w_planes[:, qk, :],
+                    rhs=x_codes[:].bitcast(FP8X4),
+                    rhs_scale=x_planes[:],
+                    start=True,
+                    stop=True,
+                )
+
         def add_bias(g):
             v_t = stream.tile([P, 2, GROUP * P], F32)
             v_t_tiles[g] = v_t
@@ -277,10 +292,11 @@ def tile_multiheadattention_pa_t_kernel(
                 )
 
         def transpose_back(g):
-            v_banks[g] = []
             for half in range(HALVES):
-                v = psum.tile([P, HALF, 2, HD], F32, tag="v", bufs=4)
-                v_banks[g].append(v)
+                if half == 1:
+                    bank = psum.tile([P, HALF, 2, HD], F32, tag="v", bufs=4)
+                    v_banks[g].append(bank)
+                v = v_banks[g][half]
                 for s in range(HALF):
                     for qk in range(2):
                         col = (half * HALF + s) * P
@@ -342,8 +358,13 @@ def tile_multiheadattention_pa_t_kernel(
 
         def store(g):
             t, j0 = groups[g]
-            for qk in range(2):
-                nc.sync.dma_start(out=out_frames[qk][t, :, j0 : j0 + GROUP, :], in_=rotated_tiles[g][:, qk, :, :])
+            pieces = HALVES if g == last else 1
+            for i in range(pieces):
+                slots = slice(i * GROUP // pieces, (i + 1) * GROUP // pieces)
+                for qk in range(2):
+                    nc.sync.dma_start(
+                        out=out_frames[qk][t, :, j0:, :][:, slots, :], in_=rotated_tiles[g][:, qk, slots, :]
+                    )
 
         def when(g, stage, *args):
             if 0 <= g < n_groups:
@@ -369,6 +390,7 @@ def tile_multiheadattention_pa_t_kernel(
                 for qk in range(2):
                     table_piece(nc.vector, qk, 0, half, True)
             transpose_x(2)
+            keep_clock(0)
             for step in range(n_groups + 2):
                 when(step + LOADS_AHEAD, load)
                 when(step, add_bias)
@@ -383,5 +405,6 @@ def tile_multiheadattention_pa_t_kernel(
                 when(step - 1, rotate_products, 1)
                 when(step + 1, project)
                 when(step + 3, transpose_x)
+                when(step + 1, keep_clock)
                 when(step - 1, rotate_add)
                 when(step - 1, store)

@@ -94,16 +94,18 @@ def tile_multiheadattention_pa_t_kernel(
         load_rows(0, H_COLS, freqs_h.rearrange("h a b -> h (a b)"))
         load_rows(0, slice(GAIN_COLS.start, GAIN_COLS.start + HD), q_scale.unsqueeze(0))
         load_rows(0, slice(GAIN_COLS.start + HD, GAIN_COLS.stop), k_scale.unsqueeze(0))
-        load_rows(0, T_COLS, freqs_t.rearrange("t a b -> (t a b)").unsqueeze(0))
         load(1)
         load_rows(0, BIAS_COLS, bq.unsqueeze(0))
         load_rows(1, BIAS_COLS, bk.unsqueeze(0))
         load_weight(0, Wq_words, Wq_scales)
-        load_weight(1, Wk_words, Wk_scales)
         load(2)
+        load_rows(0, T_COLS, freqs_t.rearrange("t a b -> (t a b)").unsqueeze(0))
+        load_weight(1, Wk_words, Wk_scales)
         load(3)
         load(4)
         load(5)
+        zeros = consts.tile([P, GROUP * P], BF16)
+        nc.vector.memset(zeros[:].bitcast(I32), 0)
         ident = consts.tile([P, P], F32)
         make_identity(nc, ident[:])
 
@@ -238,7 +240,7 @@ def tile_multiheadattention_pa_t_kernel(
             grouped_tiles[g] = grouped
             words = grouped[:].bitcast(F32).rearrange("p (h n u) -> p h n u", h=HALVES, u=2)
             for half in range(HALVES):
-                copy = nc.vector.tensor_copy if half == 1 and g > 2 else nc.scalar.copy
+                copy = nc.vector.tensor_copy if half == 1 and g > 2 and g % 4 != 0 else nc.scalar.copy
                 copy(out=words[:, half, :, :], in_=x_t_banks[g][half][:].rearrange("p u n -> p n u"))
 
         def quantise_x(g):
@@ -304,17 +306,18 @@ def tile_multiheadattention_pa_t_kernel(
 
         last = n_groups - 1
 
-        def norm(g, half):
+        def norm(g, half, slots=(0, 1)):
             squares = stream.tile([P, HALF, 2, HD], BF16, bufs=2)
-            sumsq = stream.tile([P, HALF, 2], F32, bufs=4)
-            sumsq_tiles[g, half] = sumsq
-            for s in range(HALF):
+            if 0 in slots:
+                sumsq = stream.tile([P, HALF, 2], F32, bufs=4)
+                sumsq_tiles[g, half] = sumsq
+            for s in slots:
                 for qk in range(2):
                     nc.scalar.activation(
                         out=squares[:, s, qk, :],
                         in_=v_banks[g][half][:, s, qk, :],
                         func=ACT.Square,
-                        accum_out=sumsq[:, s, qk : qk + 1],
+                        accum_out=sumsq_tiles[g, half][:, s, qk : qk + 1],
                     )
 
         def inverse_rms(g, half):
@@ -370,7 +373,13 @@ def tile_multiheadattention_pa_t_kernel(
             if 0 <= g < n_groups:
                 stage(g, *args)
 
+        def warm_up(count):
+            bank = psum.tile([P, GROUP * P], F32, tag="acc", bufs=2)
+            for i in range(count):
+                nc.tensor.matmul(bank[:], lhsT=zeros[:, 0:P], rhs=zeros[:], start=True, stop=True)
+
         with tc.manual_schedule():
+            warm_up(3)
             transpose_x(0)
             copy_x(0)
             quantise_x(0)
@@ -395,11 +404,12 @@ def tile_multiheadattention_pa_t_kernel(
                 when(step + LOADS_AHEAD, load)
                 when(step, add_bias)
                 when(step - 1, inverse_rms, 0)
-                when(step - 1, norm, 1)
                 when(step + 2, copy_x)
-                when(step - 1, inverse_rms, 1)
+                when(step - 1, norm, 1)
                 when(step, transpose_back)
-                when(step, norm, 0)
+                when(step, norm, 0, (0,))
+                when(step - 1, inverse_rms, 1)
+                when(step, norm, 0, (1,))
                 when(step - 1, rotate_products, 0)
                 when(step + 2, quantise_x)
                 when(step - 1, rotate_products, 1)

from contextlib import ExitStack

import concourse.mybir as mybir
from concourse.masks import make_identity

F32 = mybir.dt.float32
BF16 = mybir.dt.bfloat16
I32 = mybir.dt.int32
U32 = mybir.dt.uint32
U8 = mybir.dt.uint8
FP8X4 = mybir.dt.float8_e4m3fn_x4
ACT = mybir.ActivationFunctionType
ALU = mybir.AluOpType

P = 128
D = 512
HD = 128
PAIRS = HD // 2
FRAMES = 8
SLOTS = 8
GROUP = 4
HALF = 2
HALVES = GROUP // HALF
LOADS_AHEAD = 6
PAIRS_T = 22
PAIRS_H = 21
PAIRS_W = 21
HALF_HD = HD // 2
PAIRS_H0 = PAIRS // 2 - PAIRS_T
EPS = 1e-6

T_COLS = slice(0, FRAMES * 2 * PAIRS_T)
GAIN_COLS = slice(352, 352 + 2 * HD)
H_COLS = slice(608, 608 + 2 * PAIRS_H)
W_COLS = slice(656, 656 + SLOTS * 2 * PAIRS_W)
BIAS_COLS = slice(992, 992 + HD)
ROW_WIDTH = 992 + HD
BIAS_START = 384
H_START = 384

FLOPS = 2 * 8192 * D * 2 * HD


def tile_multiheadattention_pa_t_kernel(
    tc, x, Wq_words, Wq_scales, bq, Wk_words, Wk_scales, bk, q_scale, k_scale,
    freqs_t, freqs_h, freqs_w, out_0, out_1,
):
    nc = tc.nc
    x_frames = x.rearrange("b (t p j) d -> (b t) p j d", p=P, j=SLOTS)
    out_frames = [
        o.rearrange("b (t p j) h f -> (b t) p j (h f)", p=P, j=SLOTS) for o in (out_0, out_1)
    ]

    with ExitStack() as ctx:
        consts = ctx.enter_context(tc.tile_pool(name="consts", bufs=1))
        stream = ctx.enter_context(tc.tile_pool(name="stream", bufs=3))
        psum = ctx.enter_context(tc.psum_pool(name="psum", bufs=2))

        groups = [(t, j0) for t in range(FRAMES) for j0 in range(0, SLOTS, GROUP)]
        n_groups = len(groups)
        x_tiles = {}

        def load(g, pieces=1):
            t, j0 = groups[g]
            x_sb = stream.tile([P, GROUP, D], BF16, bufs=6)
            for i in range(pieces):
                slots = slice(i * GROUP // pieces, (i + 1) * GROUP // pieces)
                nc.sync.dma_start(out=x_sb[:, slots, :], in_=x_frames[t, :, j0:, :][:, slots, :])
            x_tiles[g] = x_sb

        load(0)

        w_codes = consts.tile([P, 2, HD], U32, align_bytes=64)
        w_planes = consts.tile([P, 2, HD], U8, align_bytes=64)
        nc.vector.memset(w_planes[:].rearrange("p a n -> p (a n)").bitcast(I32), 0)
        rows = consts.tile([P, ROW_WIDTH], BF16)
        nc.vector.memset(rows[:].bitcast(I32), 0)

        def load_weight(qk, words, scales):
            nc.sync.dma_start(
                out=w_codes[:, qk, :].bitcast(I32),
                in_=words.rearrange("g p n t -> (g p) (n t)").bitcast(I32),
            )
            for quad in range(4):
                nc.sync.dma_start(
                    out=w_planes[32 * quad : 32 * quad + 4, qk, :].bitcast(I32),
                    in_=scales[0, 4 * quad : 4 * quad + 4, :].bitcast(I32),
                )

        def load_rows(row0, columns, source):
            nc.sync.dma_start(out=rows[row0 : row0 + source.shape[0], columns], in_=source)

        load_rows(0, W_COLS, freqs_w.rearrange("(wh j) a b -> wh (j a b)", j=SLOTS))
        load_rows(0, H_COLS, freqs_h.rearrange("h a b -> h (a b)"))
        load_rows(0, slice(GAIN_COLS.start, GAIN_COLS.start + HD), q_scale.unsqueeze(0))
        load_rows(0, slice(GAIN_COLS.start + HD, GAIN_COLS.stop), k_scale.unsqueeze(0))
        load(1)
        load_rows(0, BIAS_COLS, bq.unsqueeze(0))
        load_rows(1, BIAS_COLS, bk.unsqueeze(0))
        load_weight(0, Wq_words, Wq_scales)
        load(2)
        load_rows(0, T_COLS, freqs_t.rearrange("t a b -> (t a b)").unsqueeze(0))
        load_weight(1, Wk_words, Wk_scales)
        load(3)
        load(4)
        load(5)
        zeros = consts.tile([P, GROUP * P], BF16)
        nc.vector.memset(zeros[:].bitcast(I32), 0)
        ident = consts.tile([P, P], F32)
        make_identity(nc, ident[:])

        eps_col = consts.tile([P, 1], F32)
        nc.vector.memset(eps_col[:], EPS)
        ident_bf16 = consts.tile([P, P], BF16)
        nc.vector.tensor_copy(out=ident_bf16[:], in_=ident[:])
        select_h = consts.tile([P, P], BF16)
        nc.vector.tensor_copy(
            out=select_h[:].rearrange("p (h r) -> p h r", r=4),
            in_=ident_bf16[:, 0:32].unsqueeze(2).to_broadcast([P, 32, 4]),
        )
        select_w = consts.tile([P, P], BF16)
        nc.vector.tensor_copy(
            out=select_w[:].rearrange("p (h r) -> p h r", r=4),
            in_=ident_bf16[:, 0:4].unsqueeze(1).to_broadcast([P, 32, 4]),
        )
        feature_order = consts.tile([P, P], F32)
        nc.vector.tensor_copy(
            out=feature_order[:].rearrange("p (b two pr) -> p b two pr", b=2, two=2),
            in_=ident[:].rearrange("p (b pr two) -> p b two pr", b=2, two=2),
        )
        bias_col = consts.tile([P, 2], F32)

        minus_row = consts.tile([P, 1], BF16)
        nc.vector.tensor_scalar_mul(out=minus_row[:], in0=ident_bf16[:, 0:1], scalar1=-1.0)
        spread_banks = {}

        def spread(out, selection, values):
            nc.tensor.matmul(out, lhsT=selection, rhs=values, start=True, stop=True)

        def spread_turns(bank, offset, columns, count, selection):
            given = rows[:, columns].rearrange("p (r a e) -> p r a e", r=count, e=2)
            width = 2 * (columns.stop - columns.start)
            out = bank[:, offset : offset + width].rearrange("p (r two a e) -> p r two a e", r=count, two=2, e=2)
            spread(out[:, :, 0].rearrange("p r a e -> p r (a e)"), selection, given.rearrange("p r a e -> p r (a e)"))
            for e in range(2):
                spread(out[:, :, 1, :, e], selection, given[:, :, :, 1 - e])

        def spread_halves(name, columns, count, selection):
            for half in range(2):
                bank = psum.tile([P, HALF * 2 * HD], F32, tag="v", bufs=4)
                spread_banks[name, half] = bank
                width = (columns.stop - columns.start) // 2
                start = columns.start + half * width
                spread_turns(bank, 0, slice(start, start + width), count // 2, selection)

        def spread_rows():
            first_row = ident_bf16[:, 0:1].to_broadcast([P, P])
            gains_bank = psum.tile([P, GROUP * P], F32, tag="acc", bufs=2)
            spread_banks["gains"] = gains_bank
            out = gains_bank[:].rearrange("p (q two pr e) -> p q two pr e", q=4, two=2, e=2)
            given = rows[:, GAIN_COLS].rearrange("p (q pr two) -> p q pr two", q=4, two=2)
            for e in range(2):
                spread(out[:, :, 0, :, e], first_row, given[:, :, :, 0])
            spread(out[:, :, 1, :, 0], minus_row[:].to_broadcast([P, P]), given[:, :, :, 1])
            spread(out[:, :, 1, :, 1], first_row, given[:, :, :, 1])
            spread_halves("w", W_COLS, SLOTS, select_w[:])
            h_split = H_COLS.start + 2 * PAIRS_H0
            spread_turns(spread_banks["w", 1], H_START, slice(H_COLS.start, h_split), 1, select_h[:])
            spread_turns(spread_banks["w", 1], H_START + 4 * PAIRS_H0, slice(h_split, H_COLS.stop), 1, select_h[:])
            spread(spread_banks["w", 0][:, BIAS_START : BIAS_START + 2], rows[:, BIAS_COLS], ident_bf16[:, 0:2])

        def spread_t():
            spread_halves("t", T_COLS, FRAMES, ident_bf16[:, 0:1].to_broadcast([P, P]))

        table_warm_up = consts.tile([P, 1], F32)
        nc.scalar.activation(out=table_warm_up[:], in_=eps_col[:], func=ACT.Abs_reciprocal_sqrt)

        signed_gains = consts.tile([P, 2, 2, 2, HALF_HD], F32)
        tables = consts.tile([P, FRAMES + SLOTS, 2, 2, HALF_HD], F32)

        turns = {
            name: consts.tile([P, width], BF16, name="turns_" + name)
            for name, width in (("w", SLOTS * 4 * PAIRS_W), ("h", 4 * PAIRS_H), ("t", FRAMES * 4 * PAIRS_T))
        }

        def copy_gains_hw():
            nc.scalar.copy(out=signed_gains[:].rearrange("p q b two n -> p (q b two n)"), in_=spread_banks["gains"][:])

        def copy_turns(name, width):
            for half in range(2):
                columns = slice(half * width // 2, (half + 1) * width // 2)
                nc.scalar.copy(out=turns[name][:, columns], in_=spread_banks[name, half][:, 0 : width // 2])

        def copy_t():
            copy_turns("t", FRAMES * 4 * PAIRS_T)

        def table_piece(engine, qk, part, half, direct):
            row0, name, start, first, pairs = (
                (0, "t", 0, 0, PAIRS_T),
                (0, "h", 0, PAIRS_T, PAIRS_H0),
                (FRAMES, "h", 4 * PAIRS_H0, 0, PAIRS_H - PAIRS_H0),
                (FRAMES, "w", 0, PAIRS_H - PAIRS_H0, PAIRS_W),
            )[part]
            halves = 1 if half is None else 2
            count = 8 // halves
            shape = [P, count, 2, 2 * pairs]
            columns = slice(2 * first, 2 * (first + pairs))
            row0 += (half or 0) * count
            if name == "h":
                given = turns["h"][:, start : start + 4 * pairs] if not direct else spread_banks["w", 1][:, H_START + start : H_START + start + 4 * pairs]
                given = given.rearrange("p (two n) -> p two n", two=2).unsqueeze(1).to_broadcast(shape)
            else:
                width = count * 4 * pairs
                given = spread_banks[name, half][:, 0:width] if direct else turns[name][:, (half or 0) * width : (half or 0) * width + width]
                given = given.rearrange("p (r two n) -> p r two n", r=count, two=2)
            engine.tensor_tensor(
                out=tables[:, row0 : row0 + count, qk, :, columns],
                in0=given,
                in1=signed_gains[:, qk, part // 2, :, columns].unsqueeze(1).to_broadcast(shape),
                op=ALU.mult,
            )

        x_t_banks, grouped_tiles, x_mx, acc_banks, v_t_tiles = {}, {}, {}, {}, {}
        v_banks, sumsq_tiles, rstd_tiles, product_tiles, rotated_tiles = {}, {}, {}, {}, {}

        def transpose_x(g):
            x_t_banks[g] = []
            for half in range(HALVES):
                x_t = psum.tile([P, 2, HALF * P], F32, tag="x_t", bufs=2)
                x_t_banks[g].append(x_t)
                for s in range(HALF):
                    words = x_tiles[g][:, half * HALF + s, :].bitcast(F32)
                    for u in range(2):
                        nc.tensor.transpose(
                            x_t[:, u, s * P : (s + 1) * P], words[:, u : D // 2 : 2], ident[:]
                        )

        def copy_x(g):
            grouped = stream.tile([P, GROUP * P * 4], BF16, align_bytes=64)
            grouped_tiles[g] = grouped
            words = grouped[:].bitcast(F32).rearrange("p (h n u) -> p h n u", h=HALVES, u=2)
            for half in range(HALVES):
                copy = nc.vector.tensor_copy if half == 1 and g > 2 and g % 4 != 0 else nc.scalar.copy
                copy(out=words[:, half, :, :], in_=x_t_banks[g][half][:].rearrange("p u n -> p n u"))

        def quantise_x(g):
            x_codes = stream.tile([P, GROUP * P], U32, align_bytes=64)
            x_planes = stream.tile([P, GROUP * P], U8, align_bytes=64)
            nc.vector.quantize_mx(
                out=x_codes[:].bitcast(FP8X4), scales=x_planes[:], in_=grouped_tiles[g][:]
            )
            x_mx[g] = (x_codes, x_planes)

        def project(g):
            x_codes, x_planes = x_mx[g]
            acc_banks[g] = []
            for qk in range(2):
                acc = psum.tile([P, GROUP * P], F32, tag="acc", bufs=2)
                acc_banks[g].append(acc)
                nc.tensor.matmul_mx(
                    out=acc[:],
                    lhsT=w_codes[:, qk, :].bitcast(FP8X4),
                    lhsT_scale=w_planes[:, qk, :],
                    rhs=x_codes[:].bitcast(FP8X4),
                    rhs_scale=x_planes[:],
                    start=True,
                    stop=True,
                )

        def keep_clock(g):
            x_codes, x_planes = x_mx[g]
            bank = psum.tile([P, HALF, 2, HD], F32, tag="v", bufs=4)
            v_banks[g] = [bank]
            for qk in range(2):
                nc.tensor.matmul_mx(
                    out=bank[:].rearrange("p s q f -> p (s q f)"),
                    lhsT=w_codes[:, qk, :].bitcast(FP8X4),
                    lhsT_scale=w_planes[:, qk, :],
                    rhs=x_codes[:].bitcast(FP8X4),
                    rhs_scale=x_planes[:],
                    start=True,
                    stop=True,
                )

        def add_bias(g):
            v_t = stream.tile([P, 2, GROUP * P], F32)
            v_t_tiles[g] = v_t
            for qk in range(2):
                nc.scalar.activation(
                    out=v_t[:, qk, :],
                    in_=acc_banks[g][qk][:],
                    func=ACT.Identity,
                    bias=bias_col[:, qk : qk + 1],
                )

        def transpose_back(g):
            for half in range(HALVES):
                if half == 1:
                    bank = psum.tile([P, HALF, 2, HD], F32, tag="v", bufs=4)
                    v_banks[g].append(bank)
                v = v_banks[g][half]
                for s in range(HALF):
                    for qk in range(2):
                        col = (half * HALF + s) * P
                        nc.tensor.transpose(v[:, s, qk, :], v_t_tiles[g][:, qk, col : col + P], feature_order[:])

        last = n_groups - 1

        def norm(g, half, slots=(0, 1)):
            squares = stream.tile([P, HALF, 2, HD], BF16, bufs=2)
            if 0 in slots:
                sumsq = stream.tile([P, HALF, 2], F32, bufs=4)
                sumsq_tiles[g, half] = sumsq
            for s in slots:
                for qk in range(2):
                    nc.scalar.activation(
                        out=squares[:, s, qk, :],
                        in_=v_banks[g][half][:, s, qk, :],
                        func=ACT.Square,
                        accum_out=sumsq_tiles[g, half][:, s, qk : qk + 1],
                    )

        def inverse_rms(g, half):
            rstd = stream.tile([P, HALF, 2], F32, bufs=4)
            rstd_tiles[g, half] = rstd
            nc.scalar.activation(
                out=rstd[:], in_=sumsq_tiles[g, half][:], func=ACT.Abs_reciprocal_sqrt, bias=eps_col[:, 0:1], scale=1.0 / HD
            )

        def rotate_products(g, half):
            t, j0 = groups[g]
            products = stream.tile([P, 2, HALF, 2, 2, HALF_HD], F32, bufs=3 * HALVES)
            product_tiles[g, half] = products
            for s in range(HALF):
                row = FRAMES + j0 + half * HALF + s
                for qk in range(2):
                    v = v_banks[g][half][:, s, qk, :]
                    nc.vector.scalar_tensor_tensor(
                        out=products[:, qk, s].rearrange("p b two (pr e) -> p b (two pr) e", e=2),
                        in0=v.rearrange("p (b f) -> p b f", b=2).unsqueeze(3).to_broadcast([P, 2, HALF_HD, 2]),
                        scalar=rstd_tiles[g, half][:, s, qk : qk + 1],
                        in1=tables[:, t : row + 1 : row - t, qk].rearrange("p b two (pr e) -> p b (two pr) e", e=2),
                        op0=ALU.mult,
                        op1=ALU.mult,
                    )

        def rotate_add(g):
            rotated = stream.tile([P, 2, GROUP, HD], F32)
            rotated_tiles[g] = rotated
            sums = rotated[:].rearrange("p q s (b n) -> p q s b n", b=2)
            for half in range(HALVES):
                terms = product_tiles[g, half][:].rearrange("p q s b two n -> p two q s b n")
                slots = slice(half * HALF, (half + 1) * HALF)
                if g != last:
                    nc.gpsimd.tensor_tensor(out=sums[:, :, slots], in0=terms[:, 0], in1=terms[:, 1], op=ALU.add)
                    continue
                for qk in range(2):
                    nc.vector.tensor_tensor(
                        out=sums[:, qk, slots], in0=terms[:, 0, qk], in1=terms[:, 1, qk], op=ALU.add
                    )

        def store(g):
            t, j0 = groups[g]
            pieces = HALVES if g == last else 1
            for i in range(pieces):
                slots = slice(i * GROUP // pieces, (i + 1) * GROUP // pieces)
                for qk in range(2):
                    nc.sync.dma_start(
                        out=out_frames[qk][t, :, j0:, :][:, slots, :], in_=rotated_tiles[g][:, qk, slots, :]
                    )

        def when(g, stage, *args):
            if 0 <= g < n_groups:
                stage(g, *args)

        def warm_up(count):
            bank = psum.tile([P, GROUP * P], F32, tag="acc", bufs=2)
            for i in range(count):
                nc.tensor.matmul(bank[:], lhsT=zeros[:, 0:P], rhs=zeros[:], start=True, stop=True)

        with tc.manual_schedule():
            warm_up(3)
            transpose_x(0)
            copy_x(0)
            quantise_x(0)
            transpose_x(1)
            spread_rows()
            nc.vector.tensor_copy(out=bias_col[:], in_=spread_banks["w", 0][:, BIAS_START : BIAS_START + 2])
            copy_gains_hw()
            for part in (3, 2, 1):
                for half in ((0, 1) if part == 3 else (None,)):
                    for qk in range(2):
                        table_piece(nc.vector, qk, part, half, True)
            copy_x(1)
            quantise_x(1)
            project(0)
            spread_t()
            for half in range(2):
                for qk in range(2):
                    table_piece(nc.vector, qk, 0, half, True)
            transpose_x(2)
            keep_clock(0)
            for step in range(n_groups + 2):
                when(step + LOADS_AHEAD, load)
                when(step, add_bias)
                when(step - 1, inverse_rms, 0)
                when(step + 2, copy_x)
                when(step - 1, norm, 1)
                when(step, transpose_back)
                when(step, norm, 0, (0,))
                when(step - 1, inverse_rms, 1)
                when(step, norm, 0, (1,))
                when(step - 1, rotate_products, 0)
                when(step + 2, quantise_x)
                when(step - 1, rotate_products, 1)
                when(step + 1, project)
                when(step + 3, transpose_x)
                when(step + 1, keep_clock)
                when(step - 1, rotate_add)
                when(step - 1, store)
